import numpy as np
import ml_dtypes


def mxq(x, axis, fmt="e4m3"):
    dtype, down = {"e4m3": (ml_dtypes.float8_e4m3fn, 7), "e5m2": (ml_dtypes.float8_e5m2, 14)}[fmt]
    v = np.moveaxis(np.asarray(x, np.float32).astype(ml_dtypes.bfloat16).astype(np.float64), axis, -1)
    blocks = v.reshape(v.shape[:-1] + (-1, 32))
    amax = np.abs(blocks).max(-1, keepdims=True)
    byte = np.maximum(np.where(amax > 0, np.frexp(amax)[1] - 1 + 127, 0) - down, 1)
    scale = np.exp2(byte - 127.0)
    codes = (blocks / scale).astype(np.float32).astype(dtype).astype(np.float64)
    return np.moveaxis((codes * scale).reshape(v.shape), -1, axis)


WIDE = False


def mx_kscale(k):
    if not WIDE:
        return np.ones(k)
    levels = np.array([10, -10, 5, -5, 0])
    a = np.random.permutation(np.resize(levels, k // 512 * 4)).reshape(k // 512, 4)
    idx = np.arange(k)
    return np.exp2(a[idx // 512, idx % 128 // 32])


BF16 = ml_dtypes.bfloat16


def bf(x):
    return np.asarray(x, np.float32).astype(BF16)


def f64(x):
    return np.asarray(x).astype(np.float64)


E2M1 = np.array([0.0, 0.5, 1.0, 1.5, 2.0, 3.0, 4.0, 6.0, -0.0, -0.5, -1.0, -1.5, -2.0, -3.0, -4.0, -6.0])


def pack_weight(w, fmt):
    k, n = w.shape
    w = f64(bf(w)).reshape(k // 32, 32, n)
    amax = np.abs(w).max(1)
    if fmt == "e4m3":
        byte = np.frexp(amax)[1] - 1 + 127 - 7
    else:
        mant, ex = np.frexp(amax / 6.0)
        byte = np.where(mant > 0.5, ex, ex - 1) + 127
    byte = np.clip(np.where(amax > 0, byte, 1), 1, 254)
    scaled = (w * np.exp2(127.0 - byte)[:, None, :]).reshape(k, n).astype(np.float32)
    by_word = np.ascontiguousarray(scaled.reshape(k // 512, 128, 4, n).transpose(0, 1, 3, 2))
    if fmt == "e4m3":
        words = by_word.astype(ml_dtypes.float8_e4m3fn).view(np.uint8)
    else:
        c = by_word.astype(ml_dtypes.float4_e2m1fn).view(np.uint8) & 0xF
        words = c[..., 0::2] | (c[..., 1::2] << 4)
    return np.ascontiguousarray(words), np.ascontiguousarray(byte.astype(np.uint8).reshape(k // 512, 16, n))


def unpack_weight(words, scales, fmt):
    g, p, n, _ = words.shape
    if fmt == "e4m3":
        vals = np.ascontiguousarray(words).view(ml_dtypes.float8_e4m3fn).astype(np.float64)
    else:
        nib = np.empty((g, p, n, 4), np.uint8)
        nib[..., 0::2] = words & 0xF
        nib[..., 1::2] = words >> 4
        vals = E2M1[nib]
    vals = vals * np.repeat(np.exp2(scales.astype(np.float64) - 127.0), 8, axis=1)[..., None]
    return vals.transpose(0, 1, 3, 2).reshape(g * 512, n)


NM, B, IN, H1, H2, OUT = 8, 512, 512, 512, 1024, 128
LS_LO, LS_HI = -20.0, 4.0
MIN_LS, MAX_LS = -20.0, 2.0


def fnoise(ei, ej):
    return np.sign(ei) * np.sign(ej) * np.sqrt(np.abs(ei)) * np.sqrt(np.abs(ej))


def plin(xq, w, b):
    y = xq.transpose(1, 0, 2) @ w
    return y.transpose(1, 0, 2) + f64(b)[None]


def setup_inputs():
    k = mx_kscale(H1)
    t = mx_kscale(H2)
    x1 = bf(np.maximum(np.random.standard_normal((B, NM, H1)) * 3.5, 0.0) * k)
    ei2 = bf(np.random.standard_normal((B, NM, 1)))
    ej2 = bf(np.random.standard_normal((1, NM, H2)) * t * t)
    w21 = np.random.standard_normal((NM, H2, H1)) * 0.4 / np.sqrt(H1) / k * t[:, None]
    b21 = bf(np.random.standard_normal((NM, H2)) * 0.3 * t)
    w22 = np.random.standard_normal((NM, H2, H1)) * 0.48 / np.sqrt(H1) / k
    b22 = bf(np.random.standard_normal((NM, H2)) * 0.3)
    w31 = np.random.standard_normal((NM, OUT, H2)) * 0.4 / np.sqrt(H2) / t
    b31 = bf(np.random.standard_normal((NM, OUT)) * 0.3)
    w32 = np.random.standard_normal((NM, OUT, H2)) * 2.4 / np.sqrt(H2) / t
    b32 = bf(np.random.standard_normal((NM, OUT)) * 2.0 - 9.0)
    w21_words, w21_scales = pack_weight(w21.swapaxes(1, 2).reshape(-1, H2), "e4m3")
    w22_words, w22_scales = pack_weight(w22.swapaxes(1, 2).reshape(-1, H2), "e4m3")
    w31_words, w31_scales = pack_weight(w31.swapaxes(1, 2).reshape(-1, OUT), "e4m3")
    w32_words, w32_scales = pack_weight(w32.swapaxes(1, 2).reshape(-1, OUT), "e4m3")
    return {'x1': x1,
            'ei2': ei2,
            'ej2': ej2,
            'w21_words': w21_words,
            'w21_scales': w21_scales,
            'b21': b21,
            'w22_words': w22_words,
            'w22_scales': w22_scales,
            'b22': b22,
            'w31_words': w31_words,
            'w31_scales': w31_scales,
            'b31': b31,
            'w32_words': w32_words,
            'w32_scales': w32_scales,
            'b32': b32}


def reference(x1, ei2, ej2, w21_words, w21_scales, b21, w22_words, w22_scales, b22, w31_words, w31_scales, b31, w32_words, w32_scales, b32):
    w21 = unpack_weight(w21_words, w21_scales, "e4m3").reshape(NM, H1, H2)
    w22 = unpack_weight(w22_words, w22_scales, "e4m3").reshape(NM, H1, H2)
    w31 = unpack_weight(w31_words, w31_scales, "e4m3").reshape(NM, H2, OUT)
    w32 = unpack_weight(w32_words, w32_scales, "e4m3").reshape(NM, H2, OUT)
    x1q = mxq(f64(x1), 2, 'e4m3')
    mu = plin(x1q, w21, b21)
    log_sigma = np.clip(plin(x1q, w22, b22), LS_LO, LS_HI)
    x2 = np.maximum(mu + fnoise(f64(ei2), f64(ej2)) * np.exp(log_sigma), 0.0)
    x2q = mxq(x2, 2, 'e4m3')
    m = plin(x2q, w31, b31)
    log_stdev = np.clip(plin(x2q, w32, b32), MIN_LS, MAX_LS)
    return m, log_stdev

@@ -1,0 +1,414 @@
+import math
+from contextlib import ExitStack
+
+import concourse.mybir as mybir
+from concourse.masks import make_identity
+
+F32 = mybir.dt.float32
+BF16 = mybir.dt.bfloat16
+I32 = mybir.dt.int32
+U32 = mybir.dt.uint32
+U8 = mybir.dt.uint8
+FP8X4 = mybir.dt.float8_e4m3fn_x4
+ALU = mybir.AluOpType
+ACT = mybir.ActivationFunctionType
+
+P = 128
+PACK = 4
+MODULES = 8
+ROWS = 512
+FEATURES = 512
+HIDDEN = 1024
+OUT = 128
+ROW_TILES = ROWS // P
+CHUNKS = HIDDEN // P
+HALVES = 2 * MODULES
+PAIRS = 2 * HALVES
+QUAD = 32
+
+SIGMA_MIN = math.exp(-20.0)
+SIGMA_MAX = math.exp(4.0)
+LOG_STDEV_MIN = -20.0
+LOG_STDEV_MAX = 2.0
+SQRT_SMALLEST = 2.0**-116
+
+FLOPS = 2 * MODULES * ROWS * (FEATURES * 2 * HIDDEN + HIDDEN * 2 * OUT)
+
+
+def tile_skill_net_pb_t_e_kernel(
+    tc,
+    x1,
+    ei2,
+    ej2,
+    w21_words,
+    w21_scales,
+    b21,
+    w22_words,
+    w22_scales,
+    b22,
+    w31_words,
+    w31_scales,
+    b31,
+    w32_words,
+    w32_scales,
+    b32,
+    out_0,
+    out_1,
+):
+    nc = tc.nc
+    with ExitStack() as ctx:
+        keep = ctx.enter_context(tc.tile_pool(name="keep", bufs=1))
+        two = ctx.enter_context(tc.tile_pool(name="two", bufs=2))
+        three = ctx.enter_context(tc.tile_pool(name="three", bufs=3))
+        four = ctx.enter_context(tc.tile_pool(name="four", bufs=4))
+        hidden_psum = ctx.enter_context(tc.psum_pool(name="hidden_psum", bufs=2))
+        work_psum = ctx.enter_context(tc.psum_pool(name="work_psum", bufs=4))
+
+        x1_sb = keep.tile([P, MODULES, ROW_TILES, FEATURES], BF16)
+        hidden_words = keep.tile([P, MODULES, 2, HIDDEN], I32, align_bytes=64)
+        hidden_scales = keep.tile([P, 2, MODULES // 4, HIDDEN], U8, align_bytes=64)
+        head_words = keep.tile([P, HALVES, 2, OUT], I32, align_bytes=64)
+        head_scales = keep.tile([P, HALVES, 2, OUT], U8, align_bytes=64)
+        head_bias = keep.tile([P, MODULES, 2, OUT], BF16)
+        ident = keep.tile([P, P], F32)
+        ident_bf = keep.tile([P, P], BF16)
+        sort_units = keep.tile([P, P], F32)
+        bias_rows = keep.tile([P, P], BF16)
+        noise_rows = keep.tile([P, P], BF16)
+        ei_sb = keep.tile([P, ROW_TILES, MODULES], BF16)
+        bias_cols = keep.tile([P, P], F32)
+        draw = keep.tile([P, 96], F32)
+        magnitude = keep.tile([P, 96], F32)
+        root = keep.tile([P, 96], F32)
+        sign = keep.tile([P, 96], F32)
+        noise = keep.tile([P, 96], F32)
+
+        nc.vector.memset(hidden_scales[:].bitcast(I32), 0)
+        nc.vector.memset(head_scales[:].bitcast(I32), 0)
+        nc.vector.memset(noise_rows[:], 0.0)
+
+        def load_x1(j):
+            nc.sync.dma_start(
+                out=x1_sb[:, j, :, :], in_=x1[:, j, :].rearrange("(a p) f -> p a f", p=P)
+            )
+
+        def load_hidden_words(j):
+            for w, words in ((1, w22_words), (0, w21_words)):
+                nc.sync.dma_start(
+                    out=hidden_words[:, j, w, :],
+                    in_=words[j].rearrange("p n t -> p (n t)").bitcast(I32),
+                )
+
+        def load_hidden_scales(four_modules):
+            first = 4 * four_modules
+            for w, scales in ((1, w22_scales), (0, w21_scales)):
+                for quadrant in range(4):
+                    nc.sync.dma_start(
+                        out=hidden_scales[
+                            QUAD * quadrant : QUAD * quadrant + 16, w, four_modules, :
+                        ].bitcast(I32),
+                        in_=scales[
+                            first : first + 4, 4 * quadrant : 4 * quadrant + 4, :
+                        ].bitcast(I32),
+                    )
+
+        def load_heads():
+            for w, words in ((0, w31_words), (1, w32_words)):
+                nc.sync.dma_start(
+                    out=head_words[:, :, w, :],
+                    in_=words.rearrange("g p n t -> p g (n t)").bitcast(I32),
+                )
+            for w, scales in ((0, w31_scales), (1, w32_scales)):
+                for quadrant in range(4):
+                    nc.sync.dma_start(
+                        out=head_scales[QUAD * quadrant : QUAD * quadrant + 4, :, w, :].bitcast(I32),
+                        in_=scales[:, 4 * quadrant : 4 * quadrant + 4, :]
+                        .rearrange("g r n -> r g n")
+                        .bitcast(I32),
+                    )
+            nc.sync.dma_start(out=head_bias[:, :, 0, :], in_=b31.partition_broadcast(P))
+            nc.sync.dma_start(out=head_bias[:, :, 1, :], in_=b32.partition_broadcast(P))
+
+        load_x1(0)
+        nc.sync.dma_start(out=bias_rows[0:64, :], in_=b21.rearrange("j (c m) -> (j c) m", m=P))
+        nc.sync.dma_start(out=bias_rows[64:P, :], in_=b22.rearrange("j (c m) -> (j c) m", m=P))
+        nc.sync.dma_start(out=noise_rows[0:64, :], in_=ej2.rearrange("o j (c m) -> (o j c) m", m=P))
+        nc.sync.dma_start(out=ei_sb[:], in_=ei2.rearrange("(a p) j o -> p a (j o)", p=P))
+        load_hidden_scales(0)
+        load_hidden_words(0)
+        load_x1(1)
+        load_hidden_words(1)
+        load_heads()
+        for j in (2, 3):
+            load_x1(j)
+            load_hidden_words(j)
+        load_hidden_scales(1)
+        for j in range(4, MODULES):
+            load_x1(j)
+            load_hidden_words(j)
+
+        make_identity(nc, ident[:])
+        nc.vector.tensor_copy(out=ident_bf[:], in_=ident[:])
+        nc.vector.tensor_copy(
+            out=sort_units[:].rearrange("k (t q) -> k t q", t=PACK),
+            in_=ident[:].rearrange("k (q t) -> k t q", t=PACK),
+        )
+
+        bias_psum = work_psum.tile([P, P], BF16, tag="work")
+        nc.tensor.transpose(out=bias_psum[:], in_=bias_rows[:], identity=ident_bf[:])
+        nc.vector.tensor_copy(out=bias_cols[:], in_=bias_psum[:])
+        b21_cols = bias_cols[:, 0:64]
+        b22_cols = bias_cols[:, 64:P]
+        noise_psum = work_psum.tile([P, P], BF16, tag="work")
+        nc.tensor.transpose(out=noise_psum[:], in_=noise_rows[:], identity=ident_bf[:])
+        nc.vector.tensor_copy(out=draw[:, 0:64], in_=noise_psum[:, 0:64])
+        nc.vector.tensor_copy(out=draw[:, 64:96], in_=ei_sb[:].rearrange("p a j -> p (a j)"))
+        nc.vector.scalar_tensor_tensor(
+            out=magnitude[:], in0=draw[:], scalar=-1.0, in1=draw[:], op0=ALU.mult, op1=ALU.max
+        )
+        nc.vector.tensor_scalar_max(out=magnitude[:], in0=magnitude[:], scalar1=SQRT_SMALLEST)
+        nc.scalar.activation(out=root[:], in_=magnitude[:], func=ACT.Sqrt)
+        nc.scalar.activation(out=sign[:], in_=draw[:], func=ACT.Sign)
+        nc.vector.tensor_mul(out=noise[:], in0=root[:], in1=sign[:])
+        unit_noise = noise[:, 0:64]
+        row_noise = noise[:, 64:96]
+
+        x1_grouped = {}
+        x1_codes = {}
+        x1_scales = {}
+        row_noise_all = {}
+        sigma = {}
+        x2_units = {}
+        x2_sorted = {}
+        x2_grouped = {}
+        x2_codes = {}
+        x2_scales = {}
+
+        def turn_x1(j):
+            grouped = two.tile([P, PACK * ROWS], BF16, align_bytes=64, name="x1_grouped")
+            x1_grouped[j] = grouped
+            grouped_words = grouped[:].bitcast(F32).rearrange(
+                "p (a b u) -> p a b u", a=ROW_TILES, u=2
+            )
+            for first in (0, 2):
+                turned = work_psum.tile([P, 2, 2, P], F32, tag="work")
+                for a in range(2):
+                    words = x1_sb[:, j, first + a, :].bitcast(F32)
+                    for u in range(2):
+                        nc.tensor.transpose(
+                            out=turned[:, a, u, :],
+                            in_=words[:, u : FEATURES // 2 : 2],
+                            identity=ident[:],
+                        )
+                nc.scalar.copy(
+                    out=grouped_words[:, first : first + 2, :, :],
+                    in_=turned[:].rearrange("p a u b -> p a b u"),
+                )
+            spread = work_psum.tile([P, ROWS], F32, tag="work")
+            for a in range(ROW_TILES):
+                column = row_noise[:, MODULES * a + j : MODULES * a + j + 1]
+                nc.tensor.transpose(
+                    out=spread[:, P * a : P * (a + 1)],
+                    in_=column.to_broadcast([P, P]),
+                    identity=ident[:],
+                )
+            on_all = two.tile([P, ROWS], F32, name="row_noise_all")
+            row_noise_all[j] = on_all
+            nc.scalar.copy(out=on_all[:], in_=spread[:])
+
+        def quantise_x1(j):
+            codes = two.tile([P, ROWS], U32, align_bytes=64, name="x1_codes")
+            scales = two.tile([P, ROWS], U8, align_bytes=64, name="x1_scales")
+            x1_codes[j] = codes
+            x1_scales[j] = scales
+            nc.vector.quantize_mx(
+                out=codes[:].bitcast(FP8X4), scales=scales[:], in_=x1_grouped[j][:]
+            )
+
+        def hidden_pass(acc, j, w, c):
+            units = slice(P * c, P * (c + 1))
+            nc.tensor.matmul_mx(
+                out=acc[:],
+                lhsT=hidden_words[:, j, w, units].bitcast(FP8X4),
+                lhsT_scale=hidden_scales[4 * (j % 4) : P, w, j // 4, units],
+                rhs=x1_codes[j][:].bitcast(FP8X4),
+                rhs_scale=x1_scales[j][:],
+                start=True,
+                stop=True,
+            )
+
+        def sigma_of_pair(n):
+            j, pair = divmod(n, CHUNKS // 2)
+            sig = three.tile([P, 2, ROWS], F32, name="sigma")
+            sigma[n] = sig
+            for i in range(2):
+                c = 2 * pair + i
+                acc = hidden_psum.tile([P, ROWS], F32, tag="log_sigma")
+                hidden_pass(acc, j, 1, c)
+                nc.scalar.activation(
+                    out=sig[:, i, :],
+                    in_=acc[:],
+                    func=ACT.Exp,
+                    bias=b22_cols[:, CHUNKS * j + c : CHUNKS * j + c + 1],
+                    scale=1.0,
+                )
+            nc.vector.tensor_scalar(
+                out=sig[:],
+                in0=sig[:],
+                scalar1=SIGMA_MIN,
+                scalar2=SIGMA_MAX,
+                op0=ALU.max,
+                op1=ALU.min,
+            )
+
+        def x2_of_pair(n):
+            j, pair = divmod(n, CHUNKS // 2)
+            half, late = divmod(n, 2)
+            if late == 0:
+                units_tile = three.tile([P, 4, ROWS], BF16, name="x2_units")
+                x2_units[half] = units_tile
+            accs = []
+            terms = []
+            for i in range(2):
+                acc = hidden_psum.tile([P, ROWS], F32, tag="mu")
+                hidden_pass(acc, j, 0, 2 * pair + i)
+                accs.append(acc)
+            for i in range(2):
+                col = CHUNKS * j + 2 * pair + i
+                term = four.tile([P, ROWS], F32, name="noise_term")
+                nc.vector.scalar_tensor_tensor(
+                    out=term[:],
+                    in0=sigma[n][:, i, :],
+                    scalar=unit_noise[:, col : col + 1],
+                    in1=row_noise_all[j][:],
+                    op0=ALU.mult,
+                    op1=ALU.mult,
+                )
+                terms.append(term)
+            for i in range(2):
+                col = CHUNKS * j + 2 * pair + i
+                nc.vector.scalar_tensor_tensor(
+                    out=x2_units[half][:, 2 * late + i, :],
+                    in0=accs[i][:],
+                    scalar=b21_cols[:, col : col + 1],
+                    in1=terms[i][:],
+                    op0=ALU.add,
+                    op1=ALU.add,
+                )
+
+        def rows_onto_partitions(half):
+            x2_sorted[half] = []
+            for s in range(2):
+                turned = work_psum.tile([P, 4, P], F32, tag="work")
+                for c in range(4):
+                    nc.tensor.transpose(
+                        out=turned[:, c, :],
+                        in_=x2_units[half][:, c, :].bitcast(F32)[:, P * s : P * (s + 1)],
+                        identity=sort_units[:],
+                    )
+                by_t = four.tile([P, PACK, 4, QUAD], F32, name="x2_sorted")
+                x2_sorted[half].append(by_t)
+                nc.scalar.copy(
+                    out=by_t[:], in_=turned[:].rearrange("p c (t q) -> p t c q", t=PACK)
+                )
+
+        def units_onto_partitions(half):
+            grouped = two.tile([P, PACK * ROWS], BF16, align_bytes=64, name="x2_grouped")
+            x2_grouped[half] = grouped
+            for s in range(2):
+                turned = work_psum.tile([P, PACK, P], F32, tag="work")
+                for t in range(PACK):
+                    nc.tensor.transpose(
+                        out=turned[:, t, :],
+                        in_=x2_sorted[half][s][:, t, :, :].rearrange("p c q -> p (c q)"),
+                        identity=ident[:],
+                    )
+                nc.scalar.activation(
+                    out=grouped[:, 2 * P * PACK * s : 2 * P * PACK * (s + 1)].rearrange(
+                        "p (b t) -> p b t", t=PACK
+                    ),
+                    in_=turned[:].bitcast(BF16).rearrange("p t b -> p b t"),
+                    func=ACT.Relu,
+                )
+
+        def quantise_x2(half):
+            j, g = divmod(half, 2)
+            if g == 0:
+                codes = two.tile([P, 2, ROWS], U32, align_bytes=64, name="x2_codes")
+                scales = two.tile([P, 2, ROWS], U8, align_bytes=64, name="x2_scales")
+                x2_codes[j] = codes
+                x2_scales[j] = scales
+            nc.vector.quantize_mx(
+                out=x2_codes[j][:, g, :].bitcast(FP8X4),
+                scales=x2_scales[j][:, g, :],
+                in_=x2_grouped[half][:],
+            )
+
+        def heads(j):
+            bias = head_bias[:, j, :, :].rearrange("p w n -> p (w n)").unsqueeze(1)
+            results = []
+            for first in (0, 2):
+                acc = work_psum.tile([P, 2, 2 * OUT], F32, tag="work")
+                for a in range(2):
+                    rows = slice(P * (first + a), P * (first + a + 1))
+                    for g in range(2):
+                        nc.tensor.matmul_mx(
+                            out=acc[:, a, :],
+                            lhsT=x2_codes[j][:, g, rows].bitcast(FP8X4),
+                            lhsT_scale=x2_scales[j][:, g, rows],
+                            rhs=head_words[:, 2 * j + g, :, :]
+                            .rearrange("p w n -> p (w n)")
+                            .bitcast(FP8X4),
+                            rhs_scale=head_scales[:, 2 * j + g, :, :].rearrange("p w n -> p (w n)"),
+                            start=(g == 0),
+                            stop=(g == 1),
+                        )
+                result = four.tile([P, 2, 2 * OUT], F32, name="result")
+                results.append(result)
+                nc.vector.tensor_tensor(
+                    out=result[:], in0=acc[:], in1=bias.to_broadcast([P, 2, 2 * OUT]), op=ALU.add
+                )
+            for result in results:
+                nc.vector.tensor_scalar(
+                    out=result[:, :, OUT : 2 * OUT],
+                    in0=result[:, :, OUT : 2 * OUT],
+                    scalar1=LOG_STDEV_MIN,
+                    scalar2=LOG_STDEV_MAX,
+                    op0=ALU.max,
+                    op1=ALU.min,
+                )
+            for first, result in zip((0, 2), results):
+                rows = slice(P * first, P * (first + 2))
+                nc.sync.dma_start(
+                    out=out_0[rows, j, :].rearrange("(a p) o -> p a o", p=P),
+                    in_=result[:, :, 0:OUT],
+                )
+                nc.sync.dma_start(
+                    out=out_1[rows, j, :].rearrange("(a p) o -> p a o", p=P),
+                    in_=result[:, :, OUT : 2 * OUT],
+                )
+
+        turn_x1(0)
+        quantise_x1(0)
+        for h in range(HALVES + 3):
+            if h < HALVES:
+                sigma_of_pair(2 * h)
+            if 0 <= 2 * h - 1 < PAIRS:
+                x2_of_pair(2 * h - 1)
+            if h % 2 == 1 and h // 2 + 1 < MODULES:
+                quantise_x1(h // 2 + 1)
+            if h % 2 == 0 and 0 <= h // 2 - 2:
+                heads(h // 2 - 2)
+            if 0 <= h - 2 < HALVES:
+                units_onto_partitions(h - 2)
+
+            if h < HALVES:
+                sigma_of_pair(2 * h + 1)
+            if 2 * h < PAIRS:
+                x2_of_pair(2 * h)
+            if 0 <= h - 1 < HALVES:
+                rows_onto_partitions(h - 1)
+            if 0 <= h - 2 < HALVES:
+                quantise_x2(h - 2)
+            if h % 2 == 0 and h // 2 + 1 < MODULES:
+                turn_x1(h // 2 + 1)

@@ -62,7 +62,9 @@ def tile_skill_net_pb_t_e_kernel(
         three = ctx.enter_context(tc.tile_pool(name="three", bufs=3))
         four = ctx.enter_context(tc.tile_pool(name="four", bufs=4))
         hidden_psum = ctx.enter_context(tc.psum_pool(name="hidden_psum", bufs=2))
-        work_psum = ctx.enter_context(tc.psum_pool(name="work_psum", bufs=4))
+        noise_psum_pool = ctx.enter_context(tc.psum_pool(name="noise_psum_pool", bufs=1))
+        work_psum = ctx.enter_context(tc.psum_pool(name="work_psum", bufs=3))
+        ctx.enter_context(tc.manual_schedule())
 
         x1_sb = keep.tile([P, MODULES, ROW_TILES, FEATURES], BF16)
         hidden_words = keep.tile([P, MODULES, 2, HIDDEN], I32, align_bytes=64)
@@ -204,7 +206,10 @@ def tile_skill_net_pb_t_e_kernel(
                     out=grouped_words[:, first : first + 2, :, :],
                     in_=turned[:].rearrange("p a u b -> p a b u"),
                 )
-            spread = work_psum.tile([P, ROWS], F32, tag="work")
+
+        def spread_row_noise(j):
+            spread = noise_psum_pool.tile([P, ROWS], F32, name="row_noise_all")
+            row_noise_all[j] = spread
             for a in range(ROW_TILES):
                 column = row_noise[:, MODULES * a + j : MODULES * a + j + 1]
                 nc.tensor.transpose(
@@ -212,9 +217,6 @@ def tile_skill_net_pb_t_e_kernel(
                     in_=column.to_broadcast([P, P]),
                     identity=ident[:],
                 )
-            on_all = two.tile([P, ROWS], F32, name="row_noise_all")
-            row_noise_all[j] = on_all
-            nc.scalar.copy(out=on_all[:], in_=spread[:])
 
         def quantise_x1(j):
             codes = two.tile([P, ROWS], U32, align_bytes=64, name="x1_codes")
@@ -252,13 +254,13 @@ def tile_skill_net_pb_t_e_kernel(
                     bias=b22_cols[:, CHUNKS * j + c : CHUNKS * j + c + 1],
                     scale=1.0,
                 )
-            nc.vector.tensor_scalar(
+            nc.gpsimd.tensor_scalar(
                 out=sig[:],
                 in0=sig[:],
-                scalar1=SIGMA_MIN,
-                scalar2=SIGMA_MAX,
-                op0=ALU.max,
-                op1=ALU.min,
+                scalar1=SIGMA_MAX,
+                scalar2=SIGMA_MIN,
+                op0=ALU.min,
+                op1=ALU.max,
             )
 
         def x2_of_pair(n):
@@ -390,11 +392,14 @@ def tile_skill_net_pb_t_e_kernel(
 
         turn_x1(0)
         quantise_x1(0)
+        spread_row_noise(0)
         for h in range(HALVES + 3):
             if h < HALVES:
                 sigma_of_pair(2 * h)
             if 0 <= 2 * h - 1 < PAIRS:
                 x2_of_pair(2 * h - 1)
+            if h % 2 == 0 and 1 <= h // 2 < MODULES:
+                spread_row_noise(h // 2)
             if h % 2 == 1 and h // 2 + 1 < MODULES:
                 quantise_x1(h // 2 + 1)
             if h % 2 == 0 and 0 <= h // 2 - 2:

@@ -62,8 +62,7 @@ def tile_skill_net_pb_t_e_kernel(
         three = ctx.enter_context(tc.tile_pool(name="three", bufs=3))
         four = ctx.enter_context(tc.tile_pool(name="four", bufs=4))
         hidden_psum = ctx.enter_context(tc.psum_pool(name="hidden_psum", bufs=2))
-        noise_psum_pool = ctx.enter_context(tc.psum_pool(name="noise_psum_pool", bufs=1))
-        work_psum = ctx.enter_context(tc.psum_pool(name="work_psum", bufs=3))
+        work_psum = ctx.enter_context(tc.psum_pool(name="work_psum", bufs=4))
         ctx.enter_context(tc.manual_schedule())
 
         x1_sb = keep.tile([P, MODULES, ROW_TILES, FEATURES], BF16)
@@ -206,10 +205,7 @@ def tile_skill_net_pb_t_e_kernel(
                     out=grouped_words[:, first : first + 2, :, :],
                     in_=turned[:].rearrange("p a u b -> p a b u"),
                 )
-
-        def spread_row_noise(j):
-            spread = noise_psum_pool.tile([P, ROWS], F32, name="row_noise_all")
-            row_noise_all[j] = spread
+            spread = work_psum.tile([P, ROWS], F32, tag="work")
             for a in range(ROW_TILES):
                 column = row_noise[:, MODULES * a + j : MODULES * a + j + 1]
                 nc.tensor.transpose(
@@ -217,6 +213,9 @@ def tile_skill_net_pb_t_e_kernel(
                     in_=column.to_broadcast([P, P]),
                     identity=ident[:],
                 )
+            on_all = two.tile([P, ROWS], F32, name="row_noise_all")
+            row_noise_all[j] = on_all
+            nc.scalar.copy(out=on_all[:], in_=spread[:])
 
         def quantise_x1(j):
             codes = two.tile([P, ROWS], U32, align_bytes=64, name="x1_codes")
@@ -254,13 +253,13 @@ def tile_skill_net_pb_t_e_kernel(
                     bias=b22_cols[:, CHUNKS * j + c : CHUNKS * j + c + 1],
                     scale=1.0,
                 )
-            nc.gpsimd.tensor_scalar(
+            nc.vector.tensor_scalar(
                 out=sig[:],
                 in0=sig[:],
-                scalar1=SIGMA_MAX,
-                scalar2=SIGMA_MIN,
-                op0=ALU.min,
-                op1=ALU.max,
+                scalar1=SIGMA_MIN,
+                scalar2=SIGMA_MAX,
+                op0=ALU.max,
+                op1=ALU.min,
             )
 
         def x2_of_pair(n):
@@ -392,14 +391,11 @@ def tile_skill_net_pb_t_e_kernel(
 
         turn_x1(0)
         quantise_x1(0)
-        spread_row_noise(0)
         for h in range(HALVES + 3):
             if h < HALVES:
                 sigma_of_pair(2 * h)
             if 0 <= 2 * h - 1 < PAIRS:
                 x2_of_pair(2 * h - 1)
-            if h % 2 == 0 and 1 <= h // 2 < MODULES:
-                spread_row_noise(h // 2)
             if h % 2 == 1 and h // 2 + 1 < MODULES:
                 quantise_x1(h // 2 + 1)
             if h % 2 == 0 and 0 <= h // 2 - 2:

@@ -62,8 +62,8 @@ def tile_skill_net_pb_t_e_kernel(
         three = ctx.enter_context(tc.tile_pool(name="three", bufs=3))
         four = ctx.enter_context(tc.tile_pool(name="four", bufs=4))
         hidden_psum = ctx.enter_context(tc.psum_pool(name="hidden_psum", bufs=2))
-        work_psum = ctx.enter_context(tc.psum_pool(name="work_psum", bufs=4))
-        ctx.enter_context(tc.manual_schedule())
+        noise_psum_pool = ctx.enter_context(tc.psum_pool(name="noise_psum_pool", bufs=1))
+        work_psum = ctx.enter_context(tc.psum_pool(name="work_psum", bufs=3))
 
         x1_sb = keep.tile([P, MODULES, ROW_TILES, FEATURES], BF16)
         hidden_words = keep.tile([P, MODULES, 2, HIDDEN], I32, align_bytes=64)
@@ -205,7 +205,10 @@ def tile_skill_net_pb_t_e_kernel(
                     out=grouped_words[:, first : first + 2, :, :],
                     in_=turned[:].rearrange("p a u b -> p a b u"),
                 )
-            spread = work_psum.tile([P, ROWS], F32, tag="work")
+
+        def spread_row_noise(j):
+            spread = noise_psum_pool.tile([P, ROWS], F32, name="row_noise_all")
+            row_noise_all[j] = spread
             for a in range(ROW_TILES):
                 column = row_noise[:, MODULES * a + j : MODULES * a + j + 1]
                 nc.tensor.transpose(
@@ -213,9 +216,6 @@ def tile_skill_net_pb_t_e_kernel(
                     in_=column.to_broadcast([P, P]),
                     identity=ident[:],
                 )
-            on_all = two.tile([P, ROWS], F32, name="row_noise_all")
-            row_noise_all[j] = on_all
-            nc.scalar.copy(out=on_all[:], in_=spread[:])
 
         def quantise_x1(j):
             codes = two.tile([P, ROWS], U32, align_bytes=64, name="x1_codes")
@@ -253,13 +253,13 @@ def tile_skill_net_pb_t_e_kernel(
                     bias=b22_cols[:, CHUNKS * j + c : CHUNKS * j + c + 1],
                     scale=1.0,
                 )
-            nc.vector.tensor_scalar(
+            nc.gpsimd.tensor_scalar(
                 out=sig[:],
                 in0=sig[:],
-                scalar1=SIGMA_MIN,
-                scalar2=SIGMA_MAX,
-                op0=ALU.max,
-                op1=ALU.min,
+                scalar1=SIGMA_MAX,
+                scalar2=SIGMA_MIN,
+                op0=ALU.min,
+                op1=ALU.max,
             )
 
         def x2_of_pair(n):
@@ -391,11 +391,14 @@ def tile_skill_net_pb_t_e_kernel(
 
         turn_x1(0)
         quantise_x1(0)
+        spread_row_noise(0)
         for h in range(HALVES + 3):
             if h < HALVES:
                 sigma_of_pair(2 * h)
             if 0 <= 2 * h - 1 < PAIRS:
                 x2_of_pair(2 * h - 1)
+            if h % 2 == 0 and 1 <= h // 2 < MODULES:
+                spread_row_noise(h // 2)
             if h % 2 == 1 and h // 2 + 1 < MODULES:
                 quantise_x1(h // 2 + 1)
             if h % 2 == 0 and 0 <= h // 2 - 2:

@@ -21,8 +21,8 @@ FEATURES = 512
 HIDDEN = 1024
 OUT = 128
 ROW_TILES = ROWS // P
-CHUNKS = HIDDEN // P
-HALVES = 2 * MODULES
+HALF_UNITS = PACK * P
+HALVES = MODULES * HIDDEN // HALF_UNITS
 PAIRS = 2 * HALVES
 QUAD = 32
 
@@ -62,31 +62,32 @@ def tile_skill_net_pb_t_e_kernel(
         three = ctx.enter_context(tc.tile_pool(name="three", bufs=3))
         four = ctx.enter_context(tc.tile_pool(name="four", bufs=4))
         hidden_psum = ctx.enter_context(tc.psum_pool(name="hidden_psum", bufs=2))
-        noise_psum_pool = ctx.enter_context(tc.psum_pool(name="noise_psum_pool", bufs=1))
-        work_psum = ctx.enter_context(tc.psum_pool(name="work_psum", bufs=3))
+        noise_psum_pool = ctx.enter_context(tc.psum_pool(name="noise_psum_pool", bufs=2))
+        work_psum = ctx.enter_context(tc.psum_pool(name="work_psum", bufs=2))
 
         x1_sb = keep.tile([P, MODULES, ROW_TILES, FEATURES], BF16)
-        hidden_words = keep.tile([P, MODULES, 2, HIDDEN], I32, align_bytes=64)
+        scales_loaded = keep.tile([P, 2, MODULES // 4, HIDDEN], U8, align_bytes=64)
         hidden_scales = keep.tile([P, 2, MODULES // 4, HIDDEN], U8, align_bytes=64)
         head_words = keep.tile([P, HALVES, 2, OUT], I32, align_bytes=64)
         head_scales = keep.tile([P, HALVES, 2, OUT], U8, align_bytes=64)
         head_bias = keep.tile([P, MODULES, 2, OUT], BF16)
         ident = keep.tile([P, P], F32)
         ident_bf = keep.tile([P, P], BF16)
-        sort_units = keep.tile([P, P], F32)
-        bias_rows = keep.tile([P, P], BF16)
-        noise_rows = keep.tile([P, P], BF16)
+        vector_rows = keep.tile([P, HALF_UNITS], BF16)
+        vector_rows_by_t = keep.tile([P, PACK, P], BF16)
         ei_sb = keep.tile([P, ROW_TILES, MODULES], BF16)
-        bias_cols = keep.tile([P, P], F32)
+        vector_cols = keep.tile([P, PACK, 3, HALVES], F32)
         draw = keep.tile([P, 96], F32)
         magnitude = keep.tile([P, 96], F32)
         root = keep.tile([P, 96], F32)
         sign = keep.tile([P, 96], F32)
         noise = keep.tile([P, 96], F32)
 
-        nc.vector.memset(hidden_scales[:].bitcast(I32), 0)
+        nc.vector.memset(vector_rows[:], 0.0)
+        nc.vector.memset(scales_loaded[:].bitcast(I32), 0)
         nc.vector.memset(head_scales[:].bitcast(I32), 0)
-        nc.vector.memset(noise_rows[:], 0.0)
+
+        hidden_loaded = {}
 
         def load_x1(j):
             nc.sync.dma_start(
@@ -95,8 +96,10 @@ def tile_skill_net_pb_t_e_kernel(
 
         def load_hidden_words(j):
             for w, words in ((1, w22_words), (0, w21_words)):
+                loaded = four.tile([P, HIDDEN], I32, name="loaded_%d" % w)
+                hidden_loaded[j, w] = loaded
                 nc.sync.dma_start(
-                    out=hidden_words[:, j, w, :],
+                    out=loaded[:],
                     in_=words[j].rearrange("p n t -> p (n t)").bitcast(I32),
                 )
 
@@ -105,7 +108,7 @@ def tile_skill_net_pb_t_e_kernel(
             for w, scales in ((1, w22_scales), (0, w21_scales)):
                 for quadrant in range(4):
                     nc.sync.dma_start(
-                        out=hidden_scales[
+                        out=scales_loaded[
                             QUAD * quadrant : QUAD * quadrant + 16, w, four_modules, :
                         ].bitcast(I32),
                         in_=scales[
@@ -131,9 +134,11 @@ def tile_skill_net_pb_t_e_kernel(
             nc.sync.dma_start(out=head_bias[:, :, 1, :], in_=b32.partition_broadcast(P))
 
         load_x1(0)
-        nc.sync.dma_start(out=bias_rows[0:64, :], in_=b21.rearrange("j (c m) -> (j c) m", m=P))
-        nc.sync.dma_start(out=bias_rows[64:P, :], in_=b22.rearrange("j (c m) -> (j c) m", m=P))
-        nc.sync.dma_start(out=noise_rows[0:64, :], in_=ej2.rearrange("o j (c m) -> (o j c) m", m=P))
+        for v, vector in enumerate((b21, b22, ej2.rearrange("o j l -> (o j) l"))):
+            nc.sync.dma_start(
+                out=vector_rows[HALVES * v : HALVES * (v + 1), :],
+                in_=vector.rearrange("j (h m) -> (j h) m", m=HALF_UNITS),
+            )
         nc.sync.dma_start(out=ei_sb[:], in_=ei2.rearrange("(a p) j o -> p a (j o)", p=P))
         load_hidden_scales(0)
         load_hidden_words(0)
@@ -150,19 +155,22 @@ def tile_skill_net_pb_t_e_kernel(
 
         make_identity(nc, ident[:])
         nc.vector.tensor_copy(out=ident_bf[:], in_=ident[:])
-        nc.vector.tensor_copy(
-            out=sort_units[:].rearrange("k (t q) -> k t q", t=PACK),
-            in_=ident[:].rearrange("k (q t) -> k t q", t=PACK),
-        )
 
-        bias_psum = work_psum.tile([P, P], BF16, tag="work")
-        nc.tensor.transpose(out=bias_psum[:], in_=bias_rows[:], identity=ident_bf[:])
-        nc.vector.tensor_copy(out=bias_cols[:], in_=bias_psum[:])
-        b21_cols = bias_cols[:, 0:64]
-        b22_cols = bias_cols[:, 64:P]
-        noise_psum = work_psum.tile([P, P], BF16, tag="work")
-        nc.tensor.transpose(out=noise_psum[:], in_=noise_rows[:], identity=ident_bf[:])
-        nc.vector.tensor_copy(out=draw[:, 0:64], in_=noise_psum[:, 0:64])
+        nc.vector.tensor_copy(
+            out=vector_rows_by_t[:], in_=vector_rows[:].rearrange("k (m t) -> k t m", t=PACK)
+        )
+        cols_psum = work_psum.tile([P, PACK, P], BF16, tag="work")
+        for t in range(PACK):
+            nc.tensor.transpose(
+                out=cols_psum[:, t, :], in_=vector_rows_by_t[:, t, :], identity=ident_bf[:]
+            )
+        nc.vector.tensor_copy(
+            out=vector_cols[:].rearrange("p t v c -> p t (v c)"),
+            in_=cols_psum[:, :, 0 : 3 * HALVES],
+        )
+        nc.vector.tensor_copy(
+            out=draw[:, 0:64].rearrange("p (t c) -> p t c", t=PACK), in_=vector_cols[:, :, 2, :]
+        )
         nc.vector.tensor_copy(out=draw[:, 64:96], in_=ei_sb[:].rearrange("p a j -> p (a j)"))
         nc.vector.scalar_tensor_tensor(
             out=magnitude[:], in0=draw[:], scalar=-1.0, in1=draw[:], op0=ALU.mult, op1=ALU.max
@@ -174,16 +182,34 @@ def tile_skill_net_pb_t_e_kernel(
         unit_noise = noise[:, 0:64]
         row_noise = noise[:, 64:96]
 
+        hidden_words = {}
         x1_grouped = {}
         x1_codes = {}
         x1_scales = {}
         row_noise_all = {}
         sigma = {}
         x2_units = {}
-        x2_sorted = {}
         x2_grouped = {}
         x2_codes = {}
         x2_scales = {}
+
+        def permute_scales(w, four_modules):
+            nc.vector.tensor_copy(
+                out=hidden_scales[:, w, four_modules, :].rearrange(
+                    "p (h t m) -> p h m t", t=PACK, m=P
+                ),
+                in_=scales_loaded[:, w, four_modules, :].rearrange(
+                    "p (h m t) -> p h m t", t=PACK, m=P
+                ),
+            )
+
+        def permute_words(j, w):
+            words = three.tile([P, HIDDEN], I32, align_bytes=64, name="words_%d" % w)
+            hidden_words[j, w] = words
+            nc.vector.tensor_copy(
+                out=words[:].rearrange("p (h t m) -> p h m t", t=PACK, m=P),
+                in_=hidden_loaded[j, w][:].rearrange("p (h m t) -> p h m t", t=PACK, m=P),
+            )
 
         def turn_x1(j):
             grouped = two.tile([P, PACK * ROWS], BF16, align_bytes=64, name="x1_grouped")
@@ -226,12 +252,13 @@ def tile_skill_net_pb_t_e_kernel(
                 out=codes[:].bitcast(FP8X4), scales=scales[:], in_=x1_grouped[j][:]
             )
 
-        def hidden_pass(acc, j, w, c):
-            units = slice(P * c, P * (c + 1))
+        def hidden_pass(acc, half, w, t):
+            j, h = divmod(half, 2)
+            first = HALF_UNITS * h + P * t
             nc.tensor.matmul_mx(
                 out=acc[:],
-                lhsT=hidden_words[:, j, w, units].bitcast(FP8X4),
-                lhsT_scale=hidden_scales[4 * (j % 4) : P, w, j // 4, units],
+                lhsT=hidden_words[j, w][:, first : first + P].bitcast(FP8X4),
+                lhsT_scale=hidden_scales[4 * (j % 4) : P, w, j // 4, first : first + P],
                 rhs=x1_codes[j][:].bitcast(FP8X4),
                 rhs_scale=x1_scales[j][:],
                 start=True,
@@ -239,18 +266,18 @@ def tile_skill_net_pb_t_e_kernel(
             )
 
         def sigma_of_pair(n):
-            j, pair = divmod(n, CHUNKS // 2)
-            sig = three.tile([P, 2, ROWS], F32, name="sigma")
+            half, late = divmod(n, 2)
+            sig = four.tile([P, 2, ROWS], F32, name="sigma")
             sigma[n] = sig
             for i in range(2):
-                c = 2 * pair + i
+                t = 2 * late + i
                 acc = hidden_psum.tile([P, ROWS], F32, tag="log_sigma")
-                hidden_pass(acc, j, 1, c)
+                hidden_pass(acc, half, 1, t)
                 nc.scalar.activation(
                     out=sig[:, i, :],
                     in_=acc[:],
                     func=ACT.Exp,
-                    bias=b22_cols[:, CHUNKS * j + c : CHUNKS * j + c + 1],
+                    bias=vector_cols[:, t, 1, half : half + 1],
                     scale=1.0,
                 )
             nc.gpsimd.tensor_scalar(
@@ -263,19 +290,19 @@ def tile_skill_net_pb_t_e_kernel(
             )
 
         def x2_of_pair(n):
-            j, pair = divmod(n, CHUNKS // 2)
             half, late = divmod(n, 2)
+            j = half // 2
             if late == 0:
-                units_tile = three.tile([P, 4, ROWS], BF16, name="x2_units")
+                units_tile = three.tile([P, PACK, ROWS], BF16, name="x2_units")
                 x2_units[half] = units_tile
             accs = []
             terms = []
             for i in range(2):
                 acc = hidden_psum.tile([P, ROWS], F32, tag="mu")
-                hidden_pass(acc, j, 0, 2 * pair + i)
+                hidden_pass(acc, half, 0, 2 * late + i)
                 accs.append(acc)
             for i in range(2):
-                col = CHUNKS * j + 2 * pair + i
+                col = HALVES * (2 * late + i) + half
                 term = four.tile([P, ROWS], F32, name="noise_term")
                 nc.vector.scalar_tensor_tensor(
                     out=term[:],
@@ -287,50 +314,26 @@ def tile_skill_net_pb_t_e_kernel(
                 )
                 terms.append(term)
             for i in range(2):
-                col = CHUNKS * j + 2 * pair + i
+                t = 2 * late + i
                 nc.vector.scalar_tensor_tensor(
-                    out=x2_units[half][:, 2 * late + i, :],
+                    out=x2_units[half][:, t, :],
                     in0=accs[i][:],
-                    scalar=b21_cols[:, col : col + 1],
+                    scalar=vector_cols[:, t, 0, half : half + 1],
                     in1=terms[i][:],
                     op0=ALU.add,
                     op1=ALU.add,
                 )
 
-        def rows_onto_partitions(half):
-            x2_sorted[half] = []
-            for s in range(2):
-                turned = work_psum.tile([P, 4, P], F32, tag="work")
-                for c in range(4):
-                    nc.tensor.transpose(
-                        out=turned[:, c, :],
-                        in_=x2_units[half][:, c, :].bitcast(F32)[:, P * s : P * (s + 1)],
-                        identity=sort_units[:],
-                    )
-                by_t = four.tile([P, PACK, 4, QUAD], F32, name="x2_sorted")
-                x2_sorted[half].append(by_t)
-                nc.scalar.copy(
-                    out=by_t[:], in_=turned[:].rearrange("p c (t q) -> p t c q", t=PACK)
-                )
-
-        def units_onto_partitions(half):
-            grouped = two.tile([P, PACK * ROWS], BF16, align_bytes=64, name="x2_grouped")
-            x2_grouped[half] = grouped
-            for s in range(2):
-                turned = work_psum.tile([P, PACK, P], F32, tag="work")
-                for t in range(PACK):
-                    nc.tensor.transpose(
-                        out=turned[:, t, :],
-                        in_=x2_sorted[half][s][:, t, :, :].rearrange("p c q -> p (c q)"),
-                        identity=ident[:],
-                    )
-                nc.scalar.activation(
-                    out=grouped[:, 2 * P * PACK * s : 2 * P * PACK * (s + 1)].rearrange(
-                        "p (b t) -> p b t", t=PACK
-                    ),
-                    in_=turned[:].bitcast(BF16).rearrange("p t b -> p b t"),
-                    func=ACT.Relu,
-                )
+        def relu_and_group(half, part):
+            if part == 0:
+                grouped = two.tile([P, ROWS, PACK], BF16, align_bytes=64, name="x2_grouped")
+                x2_grouped[half] = grouped
+            rows = slice(ROWS // 2 * part, ROWS // 2 * (part + 1))
+            nc.scalar.activation(
+                out=x2_grouped[half][:, rows, :],
+                in_=x2_units[half][:, :, rows].rearrange("p t b -> p b t"),
+                func=ACT.Relu,
+            )
 
         def quantise_x2(half):
             j, g = divmod(half, 2)
@@ -342,7 +345,7 @@ def tile_skill_net_pb_t_e_kernel(
             nc.vector.quantize_mx(
                 out=x2_codes[j][:, g, :].bitcast(FP8X4),
                 scales=x2_scales[j][:, g, :],
-                in_=x2_grouped[half][:],
+                in_=x2_grouped[half][:].rearrange("p b t -> p (b t)"),
             )
 
         def heads(j):
@@ -370,7 +373,7 @@ def tile_skill_net_pb_t_e_kernel(
                     out=result[:], in0=acc[:], in1=bias.to_broadcast([P, 2, 2 * OUT]), op=ALU.add
                 )
             for result in results:
-                nc.vector.tensor_scalar(
+                nc.gpsimd.tensor_scalar(
                     out=result[:, :, OUT : 2 * OUT],
                     in0=result[:, :, OUT : 2 * OUT],
                     scalar1=LOG_STDEV_MIN,
@@ -390,29 +393,40 @@ def tile_skill_net_pb_t_e_kernel(
                 )
 
         turn_x1(0)
+        permute_scales(1, 0)
+        permute_words(0, 1)
         quantise_x1(0)
+        permute_scales(0, 0)
+        permute_words(0, 0)
         spread_row_noise(0)
         for h in range(HALVES + 3):
+            j = h // 2
             if h < HALVES:
                 sigma_of_pair(2 * h)
             if 0 <= 2 * h - 1 < PAIRS:
                 x2_of_pair(2 * h - 1)
-            if h % 2 == 0 and 1 <= h // 2 < MODULES:
-                spread_row_noise(h // 2)
-            if h % 2 == 1 and h // 2 + 1 < MODULES:
-                quantise_x1(h // 2 + 1)
-            if h % 2 == 0 and 0 <= h // 2 - 2:
-                heads(h // 2 - 2)
+            if h % 2 == 0 and j + 1 < MODULES:
+                spread_row_noise(j + 1)
+                permute_words(j + 1, 1)
+                if j + 1 == 4:
+                    permute_scales(1, 1)
+            if h % 2 == 1 and j + 1 < MODULES:
+                quantise_x1(j + 1)
+                permute_words(j + 1, 0)
+                if j + 1 == 4:
+                    permute_scales(0, 1)
+            if h % 2 == 0 and 0 <= j - 2:
+                heads(j - 2)
             if 0 <= h - 2 < HALVES:
-                units_onto_partitions(h - 2)
+                quantise_x2(h - 2)
 
+            if 0 <= h - 1 < HALVES:
+                relu_and_group(h - 1, 0)
             if h < HALVES:
                 sigma_of_pair(2 * h + 1)
             if 2 * h < PAIRS:
                 x2_of_pair(2 * h)
             if 0 <= h - 1 < HALVES:
-                rows_onto_partitions(h - 1)
-            if 0 <= h - 2 < HALVES:
-                quantise_x2(h - 2)
-            if h % 2 == 0 and h // 2 + 1 < MODULES:
-                turn_x1(h // 2 + 1)
+                relu_and_group(h - 1, 1)
+            if h % 2 == 0 and j + 1 < MODULES:
+                turn_x1(j + 1)

@@ -280,14 +280,14 @@ def tile_skill_net_pb_t_e_kernel(
                     bias=vector_cols[:, t, 1, half : half + 1],
                     scale=1.0,
                 )
-            nc.gpsimd.tensor_scalar(
-                out=sig[:],
-                in0=sig[:],
-                scalar1=SIGMA_MAX,
-                scalar2=SIGMA_MIN,
-                op0=ALU.min,
-                op1=ALU.max,
-            )
+                nc.gpsimd.tensor_scalar(
+                    out=sig[:, i, :],
+                    in0=sig[:, i, :],
+                    scalar1=SIGMA_MAX,
+                    scalar2=SIGMA_MIN,
+                    op0=ALU.min,
+                    op1=ALU.max,
+                )
 
         def x2_of_pair(n):
             half, late = divmod(n, 2)
@@ -373,7 +373,7 @@ def tile_skill_net_pb_t_e_kernel(
                     out=result[:], in0=acc[:], in1=bias.to_broadcast([P, 2, 2 * OUT]), op=ALU.add
                 )
             for result in results:
-                nc.gpsimd.tensor_scalar(
+                nc.vector.tensor_scalar(
                     out=result[:, :, OUT : 2 * OUT],
                     in0=result[:, :, OUT : 2 * OUT],
                     scalar1=LOG_STDEV_MIN,

@@ -70,7 +70,9 @@ def tile_skill_net_pb_t_e_kernel(
         hidden_scales = keep.tile([P, 2, MODULES // 4, HIDDEN], U8, align_bytes=64)
         head_words = keep.tile([P, HALVES, 2, OUT], I32, align_bytes=64)
         head_scales = keep.tile([P, HALVES, 2, OUT], U8, align_bytes=64)
-        head_bias = keep.tile([P, MODULES, 2, OUT], BF16)
+        last_bias = keep.tile([P, 2, OUT], BF16)
+        head_rows = keep.tile([P, P], BF16)
+        head_cols = keep.tile([P, 2 * MODULES], F32)
         ident = keep.tile([P, P], F32)
         ident_bf = keep.tile([P, P], BF16)
         vector_rows = keep.tile([P, HALF_UNITS], BF16)
@@ -86,6 +88,7 @@ def tile_skill_net_pb_t_e_kernel(
         nc.vector.memset(vector_rows[:], 0.0)
         nc.vector.memset(scales_loaded[:].bitcast(I32), 0)
         nc.vector.memset(head_scales[:].bitcast(I32), 0)
+        nc.vector.memset(head_rows[:], 0.0)
 
         hidden_loaded = {}
 
@@ -130,8 +133,13 @@ def tile_skill_net_pb_t_e_kernel(
                         .rearrange("g r n -> r g n")
                         .bitcast(I32),
                     )
-            nc.sync.dma_start(out=head_bias[:, :, 0, :], in_=b31.partition_broadcast(P))
-            nc.sync.dma_start(out=head_bias[:, :, 1, :], in_=b32.partition_broadcast(P))
+            for w, vector in ((0, b31), (1, b32)):
+                nc.sync.dma_start(
+                    out=head_rows[MODULES * w : MODULES * (w + 1), :], in_=vector[:, :]
+                )
+                nc.sync.dma_start(
+                    out=last_bias[:, w, :], in_=vector[MODULES - 1, :].partition_broadcast(P)
+                )
 
         load_x1(0)
         for v, vector in enumerate((b21, b22, ej2.rearrange("o j l -> (o j) l"))):
@@ -192,6 +200,7 @@ def tile_skill_net_pb_t_e_kernel(
         x2_grouped = {}
         x2_codes = {}
         x2_scales = {}
+        by_output = {}
 
         def permute_scales(w, four_modules):
             nc.vector.tensor_copy(
@@ -348,8 +357,62 @@ def tile_skill_net_pb_t_e_kernel(
                 in_=x2_grouped[half][:].rearrange("p b t -> p (b t)"),
             )
 
-        def heads(j):
-            bias = head_bias[:, j, :, :].rearrange("p w n -> p (w n)").unsqueeze(1)
+        def turn_head_bias():
+            turned = work_psum.tile([P, P], BF16, tag="work")
+            nc.tensor.transpose(out=turned[:], in_=head_rows[:], identity=ident_bf[:])
+            nc.vector.tensor_copy(out=head_cols[:], in_=turned[:, 0 : 2 * MODULES])
+
+        def heads_by_output(j):
+            by_output[j] = []
+            for w in range(2):
+                acc = work_psum.tile([P, ROWS], F32, tag="work")
+                for g in range(2):
+                    nc.tensor.matmul_mx(
+                        out=acc[:],
+                        lhsT=head_words[:, 2 * j + g, w, :].bitcast(FP8X4),
+                        lhsT_scale=head_scales[:, 2 * j + g, w, :],
+                        rhs=x2_codes[j][:, g, :].bitcast(FP8X4),
+                        rhs_scale=x2_scales[j][:, g, :],
+                        start=(g == 0),
+                        stop=(g == 1),
+                    )
+                outputs = two.tile([P, ROWS], F32, name="outputs_%d" % w)
+                by_output[j].append(outputs)
+                nc.scalar.activation(
+                    out=outputs[:],
+                    in_=acc[:],
+                    func=ACT.Identity,
+                    bias=head_cols[:, MODULES * w + j : MODULES * w + j + 1],
+                    scale=1.0,
+                )
+                if w == 1:
+                    nc.gpsimd.tensor_scalar(
+                        out=outputs[:],
+                        in0=outputs[:],
+                        scalar1=LOG_STDEV_MAX,
+                        scalar2=LOG_STDEV_MIN,
+                        op0=ALU.min,
+                        op1=ALU.max,
+                    )
+
+        def store_heads(j):
+            for w, out in ((0, out_0), (1, out_1)):
+                turned = work_psum.tile([P, ROW_TILES, OUT], F32, tag="work")
+                for a in range(ROW_TILES):
+                    nc.tensor.transpose(
+                        out=turned[:, a, :],
+                        in_=by_output[j][w][:, P * a : P * (a + 1)],
+                        identity=ident[:],
+                    )
+                by_row = two.tile([P, ROW_TILES, OUT], F32, name="by_row_%d" % w)
+                nc.scalar.copy(out=by_row[:], in_=turned[:])
+                nc.sync.dma_start(
+                    out=out[:, j, :].rearrange("(a p) o -> p a o", p=P), in_=by_row[:]
+                )
+
+        def last_heads():
+            j = MODULES - 1
+            bias = last_bias[:].rearrange("p w n -> p (w n)").unsqueeze(1)
             results = []
             for first in (0, 2):
                 acc = work_psum.tile([P, 2, 2 * OUT], F32, tag="work")
@@ -367,7 +430,7 @@ def tile_skill_net_pb_t_e_kernel(
                             start=(g == 0),
                             stop=(g == 1),
                         )
-                result = four.tile([P, 2, 2 * OUT], F32, name="result")
+                result = two.tile([P, 2, 2 * OUT], F32, name="result")
                 results.append(result)
                 nc.vector.tensor_tensor(
                     out=result[:], in0=acc[:], in1=bias.to_broadcast([P, 2, 2 * OUT]), op=ALU.add
@@ -415,8 +478,15 @@ def tile_skill_net_pb_t_e_kernel(
                 permute_words(j + 1, 0)
                 if j + 1 == 4:
                     permute_scales(0, 1)
+            if h == 2:
+                turn_head_bias()
+            if h % 2 == 1 and 0 <= j - 2 < MODULES - 1:
+                store_heads(j - 2)
             if h % 2 == 0 and 0 <= j - 2:
-                heads(j - 2)
+                if j - 2 < MODULES - 1:
+                    heads_by_output(j - 2)
+                else:
+                    last_heads()
             if 0 <= h - 2 < HALVES:
                 quantise_x2(h - 2)
 

@@ -25,6 +25,7 @@ HALF_UNITS = PACK * P
 HALVES = MODULES * HIDDEN // HALF_UNITS
 PAIRS = 2 * HALVES
 QUAD = 32
+GROUP_ROWS = 4
 
 SIGMA_MIN = math.exp(-20.0)
 SIGMA_MAX = math.exp(4.0)
@@ -76,19 +77,24 @@ def tile_skill_net_pb_t_e_kernel(
         ident = keep.tile([P, P], F32)
         ident_bf = keep.tile([P, P], BF16)
         vector_rows = keep.tile([P, HALF_UNITS], BF16)
-        vector_rows_by_t = keep.tile([P, PACK, P], BF16)
+        vector_rows_by_t = keep.tile([P, PACK, P], F32)
         ei_sb = keep.tile([P, ROW_TILES, MODULES], BF16)
         vector_cols = keep.tile([P, PACK, 3, HALVES], F32)
-        draw = keep.tile([P, 96], F32)
         magnitude = keep.tile([P, 96], F32)
         root = keep.tile([P, 96], F32)
         sign = keep.tile([P, 96], F32)
+        table = keep.tile([P, 1], F32)
         noise = keep.tile([P, 96], F32)
 
+        nc.vector.memset(table[:], 1.0)
+        nc.scalar.activation(out=table[:], in_=table[:], func=ACT.Sqrt)
+
         nc.vector.memset(vector_rows[:], 0.0)
-        nc.vector.memset(scales_loaded[:].bitcast(I32), 0)
-        nc.vector.memset(head_scales[:].bitcast(I32), 0)
-        nc.vector.memset(head_rows[:], 0.0)
+        nc.vector.memset(scales_loaded[:, 1, :, :].bitcast(I32), 0)
+        nc.vector.memset(scales_loaded[:, 0, :, :].bitcast(I32), 0)
+        make_identity(nc, ident[:])
+        nc.gpsimd.memset(head_rows[:], 0.0)
+        nc.gpsimd.memset(head_scales[:].bitcast(I32), 0)
 
         hidden_loaded = {}
 
@@ -97,27 +103,27 @@ def tile_skill_net_pb_t_e_kernel(
                 out=x1_sb[:, j, :, :], in_=x1[:, j, :].rearrange("(a p) f -> p a f", p=P)
             )
 
-        def load_hidden_words(j):
-            for w, words in ((1, w22_words), (0, w21_words)):
-                loaded = four.tile([P, HIDDEN], I32, name="loaded_%d" % w)
-                hidden_loaded[j, w] = loaded
-                nc.sync.dma_start(
-                    out=loaded[:],
-                    in_=words[j].rearrange("p n t -> p (n t)").bitcast(I32),
-                )
+        def load_hidden_words(j, w):
+            words = (w21_words, w22_words)[w]
+            loaded = four.tile([P, HIDDEN], I32, name="loaded_%d" % w)
+            hidden_loaded[j, w] = loaded
+            nc.sync.dma_start(
+                out=loaded[:],
+                in_=words[j].rearrange("p n t -> p (n t)").bitcast(I32),
+            )
 
-        def load_hidden_scales(four_modules):
+        def load_hidden_scales(four_modules, w):
+            scales = (w21_scales, w22_scales)[w]
             first = 4 * four_modules
-            for w, scales in ((1, w22_scales), (0, w21_scales)):
-                for quadrant in range(4):
-                    nc.sync.dma_start(
-                        out=scales_loaded[
-                            QUAD * quadrant : QUAD * quadrant + 16, w, four_modules, :
-                        ].bitcast(I32),
-                        in_=scales[
-                            first : first + 4, 4 * quadrant : 4 * quadrant + 4, :
-                        ].bitcast(I32),
-                    )
+            for quadrant in range(4):
+                nc.sync.dma_start(
+                    out=scales_loaded[
+                        QUAD * quadrant : QUAD * quadrant + 16, w, four_modules, :
+                    ].bitcast(I32),
+                    in_=scales[
+                        first : first + 4, 4 * quadrant : 4 * quadrant + 4, :
+                    ].bitcast(I32),
+                )
 
         def load_heads():
             for w, words in ((0, w31_words), (1, w32_words)):
@@ -142,53 +148,26 @@ def tile_skill_net_pb_t_e_kernel(
                 )
 
         load_x1(0)
-        for v, vector in enumerate((b21, b22, ej2.rearrange("o j l -> (o j) l"))):
+        for v, vector in ((2, ej2.rearrange("o j l -> (o j) l")), (1, b22), (0, b21)):
             nc.sync.dma_start(
                 out=vector_rows[HALVES * v : HALVES * (v + 1), :],
                 in_=vector.rearrange("j (h m) -> (j h) m", m=HALF_UNITS),
             )
         nc.sync.dma_start(out=ei_sb[:], in_=ei2.rearrange("(a p) j o -> p a (j o)", p=P))
-        load_hidden_scales(0)
-        load_hidden_words(0)
+        for w in (1, 0):
+            load_hidden_scales(0, w)
+            load_hidden_words(0, w)
         load_x1(1)
-        load_hidden_words(1)
+        for w in (1, 0):
+            load_hidden_words(1, w)
         load_heads()
-        for j in (2, 3):
+        for j in range(2, MODULES):
             load_x1(j)
-            load_hidden_words(j)
-        load_hidden_scales(1)
-        for j in range(4, MODULES):
-            load_x1(j)
-            load_hidden_words(j)
-
-        make_identity(nc, ident[:])
-        nc.vector.tensor_copy(out=ident_bf[:], in_=ident[:])
-
-        nc.vector.tensor_copy(
-            out=vector_rows_by_t[:], in_=vector_rows[:].rearrange("k (m t) -> k t m", t=PACK)
-        )
-        cols_psum = work_psum.tile([P, PACK, P], BF16, tag="work")
-        for t in range(PACK):
-            nc.tensor.transpose(
-                out=cols_psum[:, t, :], in_=vector_rows_by_t[:, t, :], identity=ident_bf[:]
-            )
-        nc.vector.tensor_copy(
-            out=vector_cols[:].rearrange("p t v c -> p t (v c)"),
-            in_=cols_psum[:, :, 0 : 3 * HALVES],
-        )
-        nc.vector.tensor_copy(
-            out=draw[:, 0:64].rearrange("p (t c) -> p t c", t=PACK), in_=vector_cols[:, :, 2, :]
-        )
-        nc.vector.tensor_copy(out=draw[:, 64:96], in_=ei_sb[:].rearrange("p a j -> p (a j)"))
-        nc.vector.scalar_tensor_tensor(
-            out=magnitude[:], in0=draw[:], scalar=-1.0, in1=draw[:], op0=ALU.mult, op1=ALU.max
-        )
-        nc.vector.tensor_scalar_max(out=magnitude[:], in0=magnitude[:], scalar1=SQRT_SMALLEST)
-        nc.scalar.activation(out=root[:], in_=magnitude[:], func=ACT.Sqrt)
-        nc.scalar.activation(out=sign[:], in_=draw[:], func=ACT.Sign)
-        nc.vector.tensor_mul(out=noise[:], in0=root[:], in1=sign[:])
-        unit_noise = noise[:, 0:64]
-        row_noise = noise[:, 64:96]
+            for w in (1, 0):
+                load_hidden_words(j, w)
+            if j == 3:
+                for w in (1, 0):
+                    load_hidden_scales(1, w)
 
         hidden_words = {}
         x1_grouped = {}
@@ -201,6 +180,42 @@ def tile_skill_net_pb_t_e_kernel(
         x2_codes = {}
         x2_scales = {}
         by_output = {}
+
+        def turn_vectors():
+            nc.vector.tensor_copy(
+                out=vector_rows_by_t[:], in_=vector_rows[:].rearrange("k (m t) -> k t m", t=PACK)
+            )
+            cols_psum = work_psum.tile([P, PACK, P], F32, tag="work")
+            for t in range(PACK):
+                nc.tensor.transpose(
+                    out=cols_psum[:, t, :], in_=vector_rows_by_t[:, t, :], identity=ident[:]
+                )
+            nc.vector.tensor_copy(
+                out=vector_cols[:].rearrange("p t v c -> p t (v c)"),
+                in_=cols_psum[:, :, 0 : 3 * HALVES],
+            )
+            draws = (vector_cols[:, :, 2, :], ei_sb[:])
+            spans = []
+            for tile in (magnitude, sign):
+                spans.append(
+                    (
+                        tile[:, 0:64].rearrange("p (t c) -> p t c", t=PACK),
+                        tile[:, 64:96].rearrange("p (a j) -> p a j", j=MODULES),
+                    )
+                )
+            for draw, out in zip(draws, spans[0]):
+                nc.vector.scalar_tensor_tensor(
+                    out=out, in0=draw, scalar=-1.0, in1=draw, op0=ALU.mult, op1=ALU.max
+                )
+            nc.vector.tensor_scalar_max(out=magnitude[:], in0=magnitude[:], scalar1=SQRT_SMALLEST)
+            nc.scalar.activation(out=root[:], in_=magnitude[:], func=ACT.Sqrt)
+            nc.scalar.activation(out=table[:], in_=root[:, 0:1], func=ACT.Exp, scale=0.0)
+            for draw, out in zip(draws, spans[1]):
+                nc.scalar.activation(out=out, in_=draw, func=ACT.Sign)
+            nc.vector.tensor_mul(out=noise[:], in0=root[:], in1=sign[:])
+
+        unit_noise = noise[:, 0:64]
+        row_noise = noise[:, 64:96]
 
         def permute_scales(w, four_modules):
             nc.vector.tensor_copy(
@@ -335,14 +350,19 @@ def tile_skill_net_pb_t_e_kernel(
 
         def relu_and_group(half, part):
             if part == 0:
-                grouped = two.tile([P, ROWS, PACK], BF16, align_bytes=64, name="x2_grouped")
-                x2_grouped[half] = grouped
+                x2_tile = two.tile([P, ROWS, PACK], BF16, align_bytes=64, name="x2_grouped")
+                x2_grouped[half] = x2_tile
             rows = slice(ROWS // 2 * part, ROWS // 2 * (part + 1))
-            nc.scalar.activation(
-                out=x2_grouped[half][:, rows, :],
-                in_=x2_units[half][:, :, rows].rearrange("p t b -> p b t"),
-                func=ACT.Relu,
+            by_row = x2_units[half][:, :, rows].rearrange(
+                "p t (c i) -> p c t i", i=GROUP_ROWS
             )
+            grouped = x2_grouped[half][:, rows, :].rearrange(
+                "p (c i) t -> p c t i", i=GROUP_ROWS
+            )
+            if half == HALVES - 1 and part == 1:
+                nc.vector.tensor_scalar_max(out=grouped, in0=by_row, scalar1=0.0)
+            else:
+                nc.scalar.activation(out=grouped, in_=by_row, func=ACT.Relu)
 
         def quantise_x2(half):
             j, g = divmod(half, 2)
@@ -351,13 +371,17 @@ def tile_skill_net_pb_t_e_kernel(
                 scales = two.tile([P, 2, ROWS], U8, align_bytes=64, name="x2_scales")
                 x2_codes[j] = codes
                 x2_scales[j] = scales
-            nc.vector.quantize_mx(
-                out=x2_codes[j][:, g, :].bitcast(FP8X4),
-                scales=x2_scales[j][:, g, :],
-                in_=x2_grouped[half][:].rearrange("p b t -> p (b t)"),
-            )
+            width = ROWS // 2 if half == HALVES - 1 else ROWS
+            for first in range(0, ROWS, width):
+                rows = slice(first, first + width)
+                nc.vector.quantize_mx(
+                    out=x2_codes[j][:, g, rows].bitcast(FP8X4),
+                    scales=x2_scales[j][:, g, rows],
+                    in_=x2_grouped[half][:, rows, :].rearrange("p b t -> p (b t)"),
+                )
 
         def turn_head_bias():
+            nc.vector.tensor_copy(out=ident_bf[:], in_=ident[:])
             turned = work_psum.tile([P, P], BF16, tag="work")
             nc.tensor.transpose(out=turned[:], in_=head_rows[:], identity=ident_bf[:])
             nc.vector.tensor_copy(out=head_cols[:], in_=turned[:, 0 : 2 * MODULES])
@@ -413,7 +437,6 @@ def tile_skill_net_pb_t_e_kernel(
         def last_heads():
             j = MODULES - 1
             bias = last_bias[:].rearrange("p w n -> p (w n)").unsqueeze(1)
-            results = []
             for first in (0, 2):
                 acc = work_psum.tile([P, 2, 2 * OUT], F32, tag="work")
                 for a in range(2):
@@ -431,11 +454,14 @@ def tile_skill_net_pb_t_e_kernel(
                             stop=(g == 1),
                         )
                 result = two.tile([P, 2, 2 * OUT], F32, name="result")
-                results.append(result)
                 nc.vector.tensor_tensor(
                     out=result[:], in0=acc[:], in1=bias.to_broadcast([P, 2, 2 * OUT]), op=ALU.add
                 )
-            for result in results:
+                rows = slice(P * first, P * (first + 2))
+                nc.sync.dma_start(
+                    out=out_0[rows, j, :].rearrange("(a p) o -> p a o", p=P),
+                    in_=result[:, :, 0:OUT],
+                )
                 nc.vector.tensor_scalar(
                     out=result[:, :, OUT : 2 * OUT],
                     in0=result[:, :, OUT : 2 * OUT],
@@ -444,17 +470,12 @@ def tile_skill_net_pb_t_e_kernel(
                     op0=ALU.max,
                     op1=ALU.min,
                 )
-            for first, result in zip((0, 2), results):
-                rows = slice(P * first, P * (first + 2))
-                nc.sync.dma_start(
-                    out=out_0[rows, j, :].rearrange("(a p) o -> p a o", p=P),
-                    in_=result[:, :, 0:OUT],
-                )
                 nc.sync.dma_start(
                     out=out_1[rows, j, :].rearrange("(a p) o -> p a o", p=P),
                     in_=result[:, :, OUT : 2 * OUT],
                 )
 
+        turn_vectors()
         turn_x1(0)
         permute_scales(1, 0)
         permute_words(0, 1)

@@ -147,13 +147,13 @@ def tile_skill_net_pb_t_e_kernel(
                     out=last_bias[:, w, :], in_=vector[MODULES - 1, :].partition_broadcast(P)
                 )
 
-        load_x1(0)
         for v, vector in ((2, ej2.rearrange("o j l -> (o j) l")), (1, b22), (0, b21)):
             nc.sync.dma_start(
                 out=vector_rows[HALVES * v : HALVES * (v + 1), :],
                 in_=vector.rearrange("j (h m) -> (j h) m", m=HALF_UNITS),
             )
         nc.sync.dma_start(out=ei_sb[:], in_=ei2.rearrange("(a p) j o -> p a (j o)", p=P))
+        load_x1(0)
         for w in (1, 0):
             load_hidden_scales(0, w)
             load_hidden_words(0, w)
@@ -185,7 +185,7 @@ def tile_skill_net_pb_t_e_kernel(
             nc.vector.tensor_copy(
                 out=vector_rows_by_t[:], in_=vector_rows[:].rearrange("k (m t) -> k t m", t=PACK)
             )
-            cols_psum = work_psum.tile([P, PACK, P], F32, tag="work")
+            cols_psum = hidden_psum.tile([P, PACK, P], F32, tag="mu")
             for t in range(PACK):
                 nc.tensor.transpose(
                     out=cols_psum[:, t, :], in_=vector_rows_by_t[:, t, :], identity=ident[:]
@@ -209,9 +209,11 @@ def tile_skill_net_pb_t_e_kernel(
                 )
             nc.vector.tensor_scalar_max(out=magnitude[:], in0=magnitude[:], scalar1=SQRT_SMALLEST)
             nc.scalar.activation(out=root[:], in_=magnitude[:], func=ACT.Sqrt)
-            nc.scalar.activation(out=table[:], in_=root[:, 0:1], func=ACT.Exp, scale=0.0)
             for draw, out in zip(draws, spans[1]):
                 nc.scalar.activation(out=out, in_=draw, func=ACT.Sign)
+
+        def finish_noise():
+            nc.scalar.activation(out=table[:], in_=root[:, 0:1], func=ACT.Exp, scale=0.0)
             nc.vector.tensor_mul(out=noise[:], in0=root[:], in1=sign[:])
 
         unit_noise = noise[:, 0:64]
@@ -475,49 +477,54 @@ def tile_skill_net_pb_t_e_kernel(
                     in_=result[:, :, OUT : 2 * OUT],
                 )
 
-        turn_vectors()
-        turn_x1(0)
-        permute_scales(1, 0)
-        permute_words(0, 1)
-        quantise_x1(0)
-        permute_scales(0, 0)
-        permute_words(0, 0)
-        spread_row_noise(0)
-        for h in range(HALVES + 3):
-            j = h // 2
-            if h < HALVES:
-                sigma_of_pair(2 * h)
-            if 0 <= 2 * h - 1 < PAIRS:
-                x2_of_pair(2 * h - 1)
-            if h % 2 == 0 and j + 1 < MODULES:
-                spread_row_noise(j + 1)
-                permute_words(j + 1, 1)
-                if j + 1 == 4:
-                    permute_scales(1, 1)
-            if h % 2 == 1 and j + 1 < MODULES:
-                quantise_x1(j + 1)
-                permute_words(j + 1, 0)
-                if j + 1 == 4:
-                    permute_scales(0, 1)
-            if h == 2:
-                turn_head_bias()
-            if h % 2 == 1 and 0 <= j - 2 < MODULES - 1:
-                store_heads(j - 2)
-            if h % 2 == 0 and 0 <= j - 2:
-                if j - 2 < MODULES - 1:
-                    heads_by_output(j - 2)
-                else:
-                    last_heads()
-            if 0 <= h - 2 < HALVES:
-                quantise_x2(h - 2)
-
-            if 0 <= h - 1 < HALVES:
-                relu_and_group(h - 1, 0)
-            if h < HALVES:
-                sigma_of_pair(2 * h + 1)
-            if 2 * h < PAIRS:
-                x2_of_pair(2 * h)
-            if 0 <= h - 1 < HALVES:
-                relu_and_group(h - 1, 1)
-            if h % 2 == 0 and j + 1 < MODULES:
-                turn_x1(j + 1)
+        with tc.manual_schedule(
+            engines={
+                mybir.EngineType.PE,
+                mybir.EngineType.DVE,
+                mybir.EngineType.Activation,
+            }
+        ):
+            turn_vectors()
+            turn_x1(0)
+            permute_scales(1, 0)
+            permute_words(0, 1)
+            finish_noise()
+            quantise_x1(0)
+            permute_scales(0, 0)
+            permute_words(0, 0)
+            for n in range(-2, PAIRS + 4):
+                j, late = divmod(n, 4)
+                if 0 <= n < PAIRS:
+                    x2_of_pair(n)
+                if n + 2 < PAIRS:
+                    sigma_of_pair(n + 2)
+                if 0 <= n - 2 < PAIRS:
+                    relu_and_group((n - 2) // 2, n % 2)
+                if n == -2:
+                    spread_row_noise(0)
+                if n == 2:
+                    turn_head_bias()
+                if late % 2 == 0 and 0 <= n // 2 - 2:
+                    quantise_x2(n // 2 - 2)
+                if late == 0 and 0 <= j and j + 1 < MODULES:
+                    quantise_x1(j + 1)
+                if late == 1:
+                    if 0 <= j and j + 1 < MODULES:
+                        permute_words(j + 1, 0)
+                        if j + 1 == 4:
+                            permute_scales(0, 1)
+                    if 0 <= j - 2 < MODULES - 1:
+                        store_heads(j - 2)
+                if late == 2:
+                    if j + 2 < MODULES:
+                        turn_x1(j + 2)
+                    if 0 <= j and j + 1 < MODULES:
+                        spread_row_noise(j + 1)
+                if late == 3:
+                    if j + 2 < MODULES:
+                        permute_words(j + 2, 1)
+                        if j + 2 == 4:
+                            permute_scales(1, 1)
+                    if 0 <= j - 1 < MODULES - 1:
+                        heads_by_output(j - 1)
+            last_heads()

@@ -62,8 +62,9 @@ def tile_skill_net_pb_t_e_kernel(
         two = ctx.enter_context(tc.tile_pool(name="two", bufs=2))
         three = ctx.enter_context(tc.tile_pool(name="three", bufs=3))
         four = ctx.enter_context(tc.tile_pool(name="four", bufs=4))
-        hidden_psum = ctx.enter_context(tc.psum_pool(name="hidden_psum", bufs=2))
-        noise_psum_pool = ctx.enter_context(tc.psum_pool(name="noise_psum_pool", bufs=2))
+        sigma_psum = ctx.enter_context(tc.psum_pool(name="sigma_psum", bufs=2))
+        mu_psum = ctx.enter_context(tc.psum_pool(name="mu_psum", bufs=3))
+        noise_psum_pool = ctx.enter_context(tc.psum_pool(name="noise_psum_pool", bufs=1))
         work_psum = ctx.enter_context(tc.psum_pool(name="work_psum", bufs=2))
 
         x1_sb = keep.tile([P, MODULES, ROW_TILES, FEATURES], BF16)
@@ -141,33 +142,32 @@ def tile_skill_net_pb_t_e_kernel(
                     )
             for w, vector in ((0, b31), (1, b32)):
                 nc.sync.dma_start(
-                    out=head_rows[MODULES * w : MODULES * (w + 1), :], in_=vector[:, :]
-                )
-                nc.sync.dma_start(
                     out=last_bias[:, w, :], in_=vector[MODULES - 1, :].partition_broadcast(P)
                 )
 
+        load_x1(0)
         for v, vector in ((2, ej2.rearrange("o j l -> (o j) l")), (1, b22), (0, b21)):
             nc.sync.dma_start(
                 out=vector_rows[HALVES * v : HALVES * (v + 1), :],
                 in_=vector.rearrange("j (h m) -> (j h) m", m=HALF_UNITS),
             )
         nc.sync.dma_start(out=ei_sb[:], in_=ei2.rearrange("(a p) j o -> p a (j o)", p=P))
-        load_x1(0)
         for w in (1, 0):
             load_hidden_scales(0, w)
             load_hidden_words(0, w)
-        load_x1(1)
-        for w in (1, 0):
-            load_hidden_words(1, w)
-        load_heads()
-        for j in range(2, MODULES):
+        for w, vector in ((0, b31), (1, b32)):
+            nc.sync.dma_start(
+                out=head_rows[MODULES * w : MODULES * (w + 1), :], in_=vector[:, :]
+            )
+        for j in range(1, MODULES):
             load_x1(j)
             for w in (1, 0):
                 load_hidden_words(j, w)
-            if j == 3:
+            if j == 2:
                 for w in (1, 0):
                     load_hidden_scales(1, w)
+            if j == 3:
+                load_heads()
 
         hidden_words = {}
         x1_grouped = {}
@@ -185,7 +185,7 @@ def tile_skill_net_pb_t_e_kernel(
             nc.vector.tensor_copy(
                 out=vector_rows_by_t[:], in_=vector_rows[:].rearrange("k (m t) -> k t m", t=PACK)
             )
-            cols_psum = hidden_psum.tile([P, PACK, P], F32, tag="mu")
+            cols_psum = mu_psum.tile([P, PACK, P], F32, tag="mu")
             for t in range(PACK):
                 nc.tensor.transpose(
                     out=cols_psum[:, t, :], in_=vector_rows_by_t[:, t, :], identity=ident[:]
@@ -237,26 +237,27 @@ def tile_skill_net_pb_t_e_kernel(
                 in_=hidden_loaded[j, w][:].rearrange("p (h m t) -> p h m t", t=PACK, m=P),
             )
 
-        def turn_x1(j):
-            grouped = two.tile([P, PACK * ROWS], BF16, align_bytes=64, name="x1_grouped")
-            x1_grouped[j] = grouped
-            grouped_words = grouped[:].bitcast(F32).rearrange(
+        def turn_x1(j, part):
+            if part == 0:
+                x1_tile = two.tile([P, PACK * ROWS], BF16, align_bytes=64, name="x1_grouped")
+                x1_grouped[j] = x1_tile
+            grouped_words = x1_grouped[j][:].bitcast(F32).rearrange(
                 "p (a b u) -> p a b u", a=ROW_TILES, u=2
             )
-            for first in (0, 2):
-                turned = work_psum.tile([P, 2, 2, P], F32, tag="work")
-                for a in range(2):
-                    words = x1_sb[:, j, first + a, :].bitcast(F32)
-                    for u in range(2):
-                        nc.tensor.transpose(
-                            out=turned[:, a, u, :],
-                            in_=words[:, u : FEATURES // 2 : 2],
-                            identity=ident[:],
-                        )
-                nc.scalar.copy(
-                    out=grouped_words[:, first : first + 2, :, :],
-                    in_=turned[:].rearrange("p a u b -> p a b u"),
-                )
+            first = 2 * part
+            turned = work_psum.tile([P, 2, 2, P], F32, tag="work")
+            for a in range(2):
+                words = x1_sb[:, j, first + a, :].bitcast(F32)
+                for u in range(2):
+                    nc.tensor.transpose(
+                        out=turned[:, a, u, :],
+                        in_=words[:, u : FEATURES // 2 : 2],
+                        identity=ident[:],
+                    )
+            nc.scalar.copy(
+                out=grouped_words[:, first : first + 2, :, :],
+                in_=turned[:].rearrange("p a u b -> p a b u"),
+            )
 
         def spread_row_noise(j):
             spread = noise_psum_pool.tile([P, ROWS], F32, name="row_noise_all")
@@ -297,7 +298,7 @@ def tile_skill_net_pb_t_e_kernel(
             sigma[n] = sig
             for i in range(2):
                 t = 2 * late + i
-                acc = hidden_psum.tile([P, ROWS], F32, tag="log_sigma")
+                acc = sigma_psum.tile([P, ROWS], F32, tag="log_sigma")
                 hidden_pass(acc, half, 1, t)
                 nc.scalar.activation(
                     out=sig[:, i, :],
@@ -324,7 +325,7 @@ def tile_skill_net_pb_t_e_kernel(
             accs = []
             terms = []
             for i in range(2):
-                acc = hidden_psum.tile([P, ROWS], F32, tag="mu")
+                acc = mu_psum.tile([P, ROWS], F32, tag="mu")
                 hidden_pass(acc, half, 0, 2 * late + i)
                 accs.append(acc)
             for i in range(2):
@@ -361,7 +362,7 @@ def tile_skill_net_pb_t_e_kernel(
             grouped = x2_grouped[half][:, rows, :].rearrange(
                 "p (c i) t -> p c t i", i=GROUP_ROWS
             )
-            if half == HALVES - 1 and part == 1:
+            if half == HALVES - 1 and part == 0:
                 nc.vector.tensor_scalar_max(out=grouped, in0=by_row, scalar1=0.0)
             else:
                 nc.scalar.activation(out=grouped, in_=by_row, func=ACT.Relu)
@@ -388,53 +389,51 @@ def tile_skill_net_pb_t_e_kernel(
             nc.tensor.transpose(out=turned[:], in_=head_rows[:], identity=ident_bf[:])
             nc.vector.tensor_copy(out=head_cols[:], in_=turned[:, 0 : 2 * MODULES])
 
-        def heads_by_output(j):
-            by_output[j] = []
-            for w in range(2):
-                acc = work_psum.tile([P, ROWS], F32, tag="work")
-                for g in range(2):
-                    nc.tensor.matmul_mx(
-                        out=acc[:],
-                        lhsT=head_words[:, 2 * j + g, w, :].bitcast(FP8X4),
-                        lhsT_scale=head_scales[:, 2 * j + g, w, :],
-                        rhs=x2_codes[j][:, g, :].bitcast(FP8X4),
-                        rhs_scale=x2_scales[j][:, g, :],
-                        start=(g == 0),
-                        stop=(g == 1),
-                    )
-                outputs = two.tile([P, ROWS], F32, name="outputs_%d" % w)
-                by_output[j].append(outputs)
-                nc.scalar.activation(
+        def head_by_output(j, w):
+            acc = work_psum.tile([P, ROWS], F32, tag="work")
+            for g in range(2):
+                nc.tensor.matmul_mx(
+                    out=acc[:],
+                    lhsT=head_words[:, 2 * j + g, w, :].bitcast(FP8X4),
+                    lhsT_scale=head_scales[:, 2 * j + g, w, :],
+                    rhs=x2_codes[j][:, g, :].bitcast(FP8X4),
+                    rhs_scale=x2_scales[j][:, g, :],
+                    start=(g == 0),
+                    stop=(g == 1),
+                )
+            outputs = two.tile([P, ROWS], F32, name="outputs_%d" % w)
+            by_output[j, w] = outputs
+            nc.scalar.activation(
+                out=outputs[:],
+                in_=acc[:],
+                func=ACT.Identity,
+                bias=head_cols[:, MODULES * w + j : MODULES * w + j + 1],
+                scale=1.0,
+            )
+            if w == 1:
+                nc.gpsimd.tensor_scalar(
                     out=outputs[:],
-                    in_=acc[:],
-                    func=ACT.Identity,
-                    bias=head_cols[:, MODULES * w + j : MODULES * w + j + 1],
-                    scale=1.0,
+                    in0=outputs[:],
+                    scalar1=LOG_STDEV_MAX,
+                    scalar2=LOG_STDEV_MIN,
+                    op0=ALU.min,
+                    op1=ALU.max,
                 )
-                if w == 1:
-                    nc.gpsimd.tensor_scalar(
-                        out=outputs[:],
-                        in0=outputs[:],
-                        scalar1=LOG_STDEV_MAX,
-                        scalar2=LOG_STDEV_MIN,
-                        op0=ALU.min,
-                        op1=ALU.max,
-                    )
 
-        def store_heads(j):
-            for w, out in ((0, out_0), (1, out_1)):
-                turned = work_psum.tile([P, ROW_TILES, OUT], F32, tag="work")
-                for a in range(ROW_TILES):
-                    nc.tensor.transpose(
-                        out=turned[:, a, :],
-                        in_=by_output[j][w][:, P * a : P * (a + 1)],
-                        identity=ident[:],
-                    )
-                by_row = two.tile([P, ROW_TILES, OUT], F32, name="by_row_%d" % w)
-                nc.scalar.copy(out=by_row[:], in_=turned[:])
-                nc.sync.dma_start(
-                    out=out[:, j, :].rearrange("(a p) o -> p a o", p=P), in_=by_row[:]
+        def store_head(j, w):
+            out = (out_0, out_1)[w]
+            turned = work_psum.tile([P, ROW_TILES, OUT], F32, tag="work")
+            for a in range(ROW_TILES):
+                nc.tensor.transpose(
+                    out=turned[:, a, :],
+                    in_=by_output[j, w][:, P * a : P * (a + 1)],
+                    identity=ident[:],
                 )
+            by_row = two.tile([P, ROW_TILES, OUT], F32, name="by_row_%d" % w)
+            nc.scalar.copy(out=by_row[:], in_=turned[:])
+            nc.sync.dma_start(
+                out=out[:, j, :].rearrange("(a p) o -> p a o", p=P), in_=by_row[:]
+            )
 
         def last_heads():
             j = MODULES - 1
@@ -484,47 +483,60 @@ def tile_skill_net_pb_t_e_kernel(
                 mybir.EngineType.Activation,
             }
         ):
+            for part in range(2):
+                turn_x1(0, part)
             turn_vectors()
-            turn_x1(0)
             permute_scales(1, 0)
             permute_words(0, 1)
             finish_noise()
+            spread_row_noise(0)
             quantise_x1(0)
-            permute_scales(0, 0)
-            permute_words(0, 0)
-            for n in range(-2, PAIRS + 4):
-                j, late = divmod(n, 4)
-                if 0 <= n < PAIRS:
-                    x2_of_pair(n)
-                if n + 2 < PAIRS:
-                    sigma_of_pair(n + 2)
-                if 0 <= n - 2 < PAIRS:
-                    relu_and_group((n - 2) // 2, n % 2)
-                if n == -2:
-                    spread_row_noise(0)
-                if n == 2:
-                    turn_head_bias()
-                if late % 2 == 0 and 0 <= n // 2 - 2:
+        permute_scales(0, 0)
+        permute_words(0, 0)
+        for n in range(-2, PAIRS + 4):
+            j, late = divmod(n, 4)
+            running = 0 <= j and j + 1 < MODULES
+            if 0 <= n < PAIRS:
+                x2_of_pair(n)
+            if n + 2 < PAIRS:
+                sigma_of_pair(n + 2)
+            if 0 <= n - 2 < PAIRS:
+                relu_and_group((n - 2) // 2, n % 2)
+            if n == -2:
+                for part in range(2):
+                    turn_x1(1, part)
+            if n == 5:
+                turn_head_bias()
+            if late == 0:
+                if 0 <= n // 2 - 2:
                     quantise_x2(n // 2 - 2)
-                if late == 0 and 0 <= j and j + 1 < MODULES:
+                if 0 <= j - 2 < MODULES - 1:
+                    head_by_output(j - 2, 1)
+                if running:
                     quantise_x1(j + 1)
-                if late == 1:
-                    if 0 <= j and j + 1 < MODULES:
-                        permute_words(j + 1, 0)
-                        if j + 1 == 4:
-                            permute_scales(0, 1)
-                    if 0 <= j - 2 < MODULES - 1:
-                        store_heads(j - 2)
-                if late == 2:
-                    if j + 2 < MODULES:
-                        turn_x1(j + 2)
-                    if 0 <= j and j + 1 < MODULES:
-                        spread_row_noise(j + 1)
-                if late == 3:
-                    if j + 2 < MODULES:
-                        permute_words(j + 2, 1)
-                        if j + 2 == 4:
-                            permute_scales(1, 1)
-                    if 0 <= j - 1 < MODULES - 1:
-                        heads_by_output(j - 1)
-            last_heads()
+            if late == 1:
+                if 0 <= j and j + 2 < MODULES:
+                    turn_x1(j + 2, 0)
+                if 0 <= j - 2 < MODULES - 1:
+                    store_head(j - 2, 0)
+                if running:
+                    permute_words(j + 1, 0)
+                    if j + 1 == 4:
+                        permute_scales(0, 1)
+            if late == 2:
+                if 0 <= n // 2 - 2:
+                    quantise_x2(n // 2 - 2)
+                if 0 <= j and j + 2 < MODULES:
+                    turn_x1(j + 2, 1)
+                if 0 <= j - 2 < MODULES - 1:
+                    store_head(j - 2, 1)
+            if late == 3:
+                if running:
+                    spread_row_noise(j + 1)
+                if 0 <= j - 1 < MODULES - 1:
+                    head_by_output(j - 1, 0)
+                if j + 2 < MODULES:
+                    permute_words(j + 2, 1)
+                    if j + 2 == 4:
+                        permute_scales(1, 1)
+        last_heads()

@@ -63,8 +63,8 @@ def tile_skill_net_pb_t_e_kernel(
         three = ctx.enter_context(tc.tile_pool(name="three", bufs=3))
         four = ctx.enter_context(tc.tile_pool(name="four", bufs=4))
         sigma_psum = ctx.enter_context(tc.psum_pool(name="sigma_psum", bufs=2))
-        mu_psum = ctx.enter_context(tc.psum_pool(name="mu_psum", bufs=3))
-        noise_psum_pool = ctx.enter_context(tc.psum_pool(name="noise_psum_pool", bufs=1))
+        mu_psum = ctx.enter_context(tc.psum_pool(name="mu_psum", bufs=2))
+        noise_psum_pool = ctx.enter_context(tc.psum_pool(name="noise_psum_pool", bufs=2))
         work_psum = ctx.enter_context(tc.psum_pool(name="work_psum", bufs=2))
 
         x1_sb = keep.tile([P, MODULES, ROW_TILES, FEATURES], BF16)
@@ -384,7 +384,6 @@ def tile_skill_net_pb_t_e_kernel(
                 )
 
         def turn_head_bias():
-            nc.vector.tensor_copy(out=ident_bf[:], in_=ident[:])
             turned = work_psum.tile([P, P], BF16, tag="work")
             nc.tensor.transpose(out=turned[:], in_=head_rows[:], identity=ident_bf[:])
             nc.vector.tensor_copy(out=head_cols[:], in_=turned[:, 0 : 2 * MODULES])
@@ -439,7 +438,7 @@ def tile_skill_net_pb_t_e_kernel(
             j = MODULES - 1
             bias = last_bias[:].rearrange("p w n -> p (w n)").unsqueeze(1)
             for first in (0, 2):
-                acc = work_psum.tile([P, 2, 2 * OUT], F32, tag="work")
+                acc = mu_psum.tile([P, 2, 2 * OUT], F32, tag="mu")
                 for a in range(2):
                     rows = slice(P * (first + a), P * (first + a + 1))
                     for g in range(2):
@@ -491,6 +490,7 @@ def tile_skill_net_pb_t_e_kernel(
             finish_noise()
             spread_row_noise(0)
             quantise_x1(0)
+        nc.vector.tensor_copy(out=ident_bf[:], in_=ident[:])
         permute_scales(0, 0)
         permute_words(0, 0)
         for n in range(-2, PAIRS + 4):
@@ -524,6 +524,8 @@ def tile_skill_net_pb_t_e_kernel(
                     if j + 1 == 4:
                         permute_scales(0, 1)
             if late == 2:
+                if running:
+                    spread_row_noise(j + 1)
                 if 0 <= n // 2 - 2:
                     quantise_x2(n // 2 - 2)
                 if 0 <= j and j + 2 < MODULES:
@@ -531,8 +533,6 @@ def tile_skill_net_pb_t_e_kernel(
                 if 0 <= j - 2 < MODULES - 1:
                     store_head(j - 2, 1)
             if late == 3:
-                if running:
-                    spread_row_noise(j + 1)
                 if 0 <= j - 1 < MODULES - 1:
                     head_by_output(j - 1, 0)
                 if j + 2 < MODULES:

@@ -62,6 +62,7 @@ def tile_skill_net_pb_t_e_kernel(
         two = ctx.enter_context(tc.tile_pool(name="two", bufs=2))
         three = ctx.enter_context(tc.tile_pool(name="three", bufs=3))
         four = ctx.enter_context(tc.tile_pool(name="four", bufs=4))
+        six = ctx.enter_context(tc.tile_pool(name="six", bufs=6))
         sigma_psum = ctx.enter_context(tc.psum_pool(name="sigma_psum", bufs=2))
         mu_psum = ctx.enter_context(tc.psum_pool(name="mu_psum", bufs=2))
         noise_psum_pool = ctx.enter_context(tc.psum_pool(name="noise_psum_pool", bufs=2))
@@ -175,6 +176,7 @@ def tile_skill_net_pb_t_e_kernel(
         x1_scales = {}
         row_noise_all = {}
         sigma = {}
+        terms = {}
         x2_units = {}
         x2_grouped = {}
         x2_codes = {}
@@ -316,21 +318,13 @@ def tile_skill_net_pb_t_e_kernel(
                     op1=ALU.max,
                 )
 
-        def x2_of_pair(n):
+        def terms_of_pair(n):
             half, late = divmod(n, 2)
             j = half // 2
-            if late == 0:
-                units_tile = three.tile([P, PACK, ROWS], BF16, name="x2_units")
-                x2_units[half] = units_tile
-            accs = []
-            terms = []
-            for i in range(2):
-                acc = mu_psum.tile([P, ROWS], F32, tag="mu")
-                hidden_pass(acc, half, 0, 2 * late + i)
-                accs.append(acc)
             for i in range(2):
                 col = HALVES * (2 * late + i) + half
-                term = four.tile([P, ROWS], F32, name="noise_term")
+                term = six.tile([P, ROWS], F32, name="noise_term")
+                terms[n, i] = term
                 nc.vector.scalar_tensor_tensor(
                     out=term[:],
                     in0=sigma[n][:, i, :],
@@ -339,14 +333,24 @@ def tile_skill_net_pb_t_e_kernel(
                     op0=ALU.mult,
                     op1=ALU.mult,
                 )
-                terms.append(term)
+
+        def x2_of_pair(n):
+            half, late = divmod(n, 2)
+            if late == 0:
+                units_tile = three.tile([P, PACK, ROWS], BF16, name="x2_units")
+                x2_units[half] = units_tile
+            accs = []
+            for i in range(2):
+                acc = mu_psum.tile([P, ROWS], F32, tag="mu")
+                hidden_pass(acc, half, 0, 2 * late + i)
+                accs.append(acc)
             for i in range(2):
                 t = 2 * late + i
                 nc.vector.scalar_tensor_tensor(
                     out=x2_units[half][:, t, :],
                     in0=accs[i][:],
                     scalar=vector_cols[:, t, 0, half : half + 1],
-                    in1=terms[i][:],
+                    in1=terms[n, i][:],
                     op0=ALU.add,
                     op1=ALU.add,
                 )
@@ -496,6 +500,8 @@ def tile_skill_net_pb_t_e_kernel(
         for n in range(-2, PAIRS + 4):
             j, late = divmod(n, 4)
             running = 0 <= j and j + 1 < MODULES
+            if 0 <= n + 1 < PAIRS:
+                terms_of_pair(n + 1)
             if 0 <= n < PAIRS:
                 x2_of_pair(n)
             if n + 2 < PAIRS:
@@ -523,9 +529,8 @@ def tile_skill_net_pb_t_e_kernel(
                     permute_words(j + 1, 0)
                     if j + 1 == 4:
                         permute_scales(0, 1)
-            if late == 2:
-                if running:
                     spread_row_noise(j + 1)
+            if late == 2:
                 if 0 <= n // 2 - 2:
                     quantise_x2(n // 2 - 2)
                 if 0 <= j and j + 2 < MODULES:

import math
from contextlib import ExitStack

import concourse.mybir as mybir
from concourse.masks import make_identity

F32 = mybir.dt.float32
BF16 = mybir.dt.bfloat16
I32 = mybir.dt.int32
U32 = mybir.dt.uint32
U8 = mybir.dt.uint8
FP8X4 = mybir.dt.float8_e4m3fn_x4
ALU = mybir.AluOpType
ACT = mybir.ActivationFunctionType

P = 128
PACK = 4
MODULES = 8
ROWS = 512
FEATURES = 512
HIDDEN = 1024
OUT = 128
ROW_TILES = ROWS // P
HALF_UNITS = PACK * P
HALVES = MODULES * HIDDEN // HALF_UNITS
PAIRS = 2 * HALVES
QUAD = 32
GROUP_ROWS = 4

SIGMA_MIN = math.exp(-20.0)
SIGMA_MAX = math.exp(4.0)
LOG_STDEV_MIN = -20.0
LOG_STDEV_MAX = 2.0
SQRT_SMALLEST = 2.0**-116

FLOPS = 2 * MODULES * ROWS * (FEATURES * 2 * HIDDEN + HIDDEN * 2 * OUT)


def tile_skill_net_pb_t_e_kernel(
    tc,
    x1,
    ei2,
    ej2,
    w21_words,
    w21_scales,
    b21,
    w22_words,
    w22_scales,
    b22,
    w31_words,
    w31_scales,
    b31,
    w32_words,
    w32_scales,
    b32,
    out_0,
    out_1,
):
    nc = tc.nc
    with ExitStack() as ctx:
        keep = ctx.enter_context(tc.tile_pool(name="keep", bufs=1))
        two = ctx.enter_context(tc.tile_pool(name="two", bufs=2))
        three = ctx.enter_context(tc.tile_pool(name="three", bufs=3))
        four = ctx.enter_context(tc.tile_pool(name="four", bufs=4))
        six = ctx.enter_context(tc.tile_pool(name="six", bufs=6))
        sigma_psum = ctx.enter_context(tc.psum_pool(name="sigma_psum", bufs=2))
        mu_psum = ctx.enter_context(tc.psum_pool(name="mu_psum", bufs=2))
        noise_psum_pool = ctx.enter_context(tc.psum_pool(name="noise_psum_pool", bufs=2))
        work_psum = ctx.enter_context(tc.psum_pool(name="work_psum", bufs=2))

        x1_sb = keep.tile([P, MODULES, ROW_TILES, FEATURES], BF16)
        scales_loaded = keep.tile([P, 2, MODULES // 4, HIDDEN], U8, align_bytes=64)
        hidden_scales = keep.tile([P, 2, MODULES // 4, HIDDEN], U8, align_bytes=64)
        head_words = keep.tile([P, HALVES, 2, OUT], I32, align_bytes=64)
        head_scales = keep.tile([P, HALVES, 2, OUT], U8, align_bytes=64)
        last_bias = keep.tile([P, 2, OUT], BF16)
        head_rows = keep.tile([P, P], BF16)
        head_cols = keep.tile([P, 2 * MODULES], F32)
        ident = keep.tile([P, P], F32)
        ident_bf = keep.tile([P, P], BF16)
        vector_rows = keep.tile([P, HALF_UNITS], BF16)
        vector_rows_by_t = keep.tile([P, PACK, P], F32)
        ei_sb = keep.tile([P, ROW_TILES, MODULES], BF16)
        vector_cols = keep.tile([P, PACK, 3, HALVES], F32)
        magnitude = keep.tile([P, 96], F32)
        root = keep.tile([P, 96], F32)
        sign = keep.tile([P, 96], F32)
        table = keep.tile([P, 1], F32)
        noise = keep.tile([P, 96], F32)

        nc.vector.memset(table[:], 1.0)
        nc.scalar.activation(out=table[:], in_=table[:], func=ACT.Sqrt)

        nc.vector.memset(vector_rows[:], 0.0)
        nc.vector.memset(scales_loaded[:, 1, :, :].bitcast(I32), 0)
        nc.vector.memset(scales_loaded[:, 0, :, :].bitcast(I32), 0)
        make_identity(nc, ident[:])
        nc.gpsimd.memset(head_rows[:], 0.0)
        nc.gpsimd.memset(head_scales[:].bitcast(I32), 0)

        hidden_loaded = {}

        def load_x1(j):
            nc.sync.dma_start(
                out=x1_sb[:, j, :, :], in_=x1[:, j, :].rearrange("(a p) f -> p a f", p=P)
            )

        def load_hidden_words(j, w):
            words = (w21_words, w22_words)[w]
            loaded = four.tile([P, HIDDEN], I32, name="loaded_%d" % w)
            hidden_loaded[j, w] = loaded
            nc.sync.dma_start(
                out=loaded[:],
                in_=words[j].rearrange("p n t -> p (n t)").bitcast(I32),
            )

        def load_hidden_scales(four_modules, w):
            scales = (w21_scales, w22_scales)[w]
            first = 4 * four_modules
            for quadrant in range(4):
                nc.sync.dma_start(
                    out=scales_loaded[
                        QUAD * quadrant : QUAD * quadrant + 16, w, four_modules, :
                    ].bitcast(I32),
                    in_=scales[
                        first : first + 4, 4 * quadrant : 4 * quadrant + 4, :
                    ].bitcast(I32),
                )

        def load_heads():
            for w, words in ((0, w31_words), (1, w32_words)):
                nc.sync.dma_start(
                    out=head_words[:, :, w, :],
                    in_=words.rearrange("g p n t -> p g (n t)").bitcast(I32),
                )
            for w, scales in ((0, w31_scales), (1, w32_scales)):
                for quadrant in range(4):
                    nc.sync.dma_start(
                        out=head_scales[QUAD * quadrant : QUAD * quadrant + 4, :, w, :].bitcast(I32),
                        in_=scales[:, 4 * quadrant : 4 * quadrant + 4, :]
                        .rearrange("g r n -> r g n")
                        .bitcast(I32),
                    )
            for w, vector in ((0, b31), (1, b32)):
                nc.sync.dma_start(
                    out=last_bias[:, w, :], in_=vector[MODULES - 1, :].partition_broadcast(P)
                )

        load_x1(0)
        for v, vector in ((2, ej2.rearrange("o j l -> (o j) l")), (1, b22), (0, b21)):
            nc.sync.dma_start(
                out=vector_rows[HALVES * v : HALVES * (v + 1), :],
                in_=vector.rearrange("j (h m) -> (j h) m", m=HALF_UNITS),
            )
        nc.sync.dma_start(out=ei_sb[:], in_=ei2.rearrange("(a p) j o -> p a (j o)", p=P))
        for w in (1, 0):
            load_hidden_scales(0, w)
            load_hidden_words(0, w)
        for w, vector in ((0, b31), (1, b32)):
            nc.sync.dma_start(
                out=head_rows[MODULES * w : MODULES * (w + 1), :], in_=vector[:, :]
            )
        for j in range(1, MODULES):
            load_x1(j)
            for w in (1, 0):
                load_hidden_words(j, w)
            if j == 2:
                for w in (1, 0):
                    load_hidden_scales(1, w)
            if j == 3:
                load_heads()

        hidden_words = {}
        x1_grouped = {}
        x1_codes = {}
        x1_scales = {}
        row_noise_all = {}
        sigma = {}
        terms = {}
        x2_units = {}
        x2_grouped = {}
        x2_codes = {}
        x2_scales = {}
        by_output = {}

        def turn_vectors():
            nc.vector.tensor_copy(
                out=vector_rows_by_t[:], in_=vector_rows[:].rearrange("k (m t) -> k t m", t=PACK)
            )
            cols_psum = mu_psum.tile([P, PACK, P], F32, tag="mu")
            for t in range(PACK):
                nc.tensor.transpose(
                    out=cols_psum[:, t, :], in_=vector_rows_by_t[:, t, :], identity=ident[:]
                )
            nc.vector.tensor_copy(
                out=vector_cols[:].rearrange("p t v c -> p t (v c)"),
                in_=cols_psum[:, :, 0 : 3 * HALVES],
            )
            draws = (vector_cols[:, :, 2, :], ei_sb[:])
            spans = []
            for tile in (magnitude, sign):
                spans.append(
                    (
                        tile[:, 0:64].rearrange("p (t c) -> p t c", t=PACK),
                        tile[:, 64:96].rearrange("p (a j) -> p a j", j=MODULES),
                    )
                )
            for draw, out in zip(draws, spans[0]):
                nc.vector.scalar_tensor_tensor(
                    out=out, in0=draw, scalar=-1.0, in1=draw, op0=ALU.mult, op1=ALU.max
                )
            nc.vector.tensor_scalar_max(out=magnitude[:], in0=magnitude[:], scalar1=SQRT_SMALLEST)
            nc.scalar.activation(out=root[:], in_=magnitude[:], func=ACT.Sqrt)
            for draw, out in zip(draws, spans[1]):
                nc.scalar.activation(out=out, in_=draw, func=ACT.Sign)

        def finish_noise():
            nc.scalar.activation(out=table[:], in_=root[:, 0:1], func=ACT.Exp, scale=0.0)
            nc.vector.tensor_mul(out=noise[:], in0=root[:], in1=sign[:])

        unit_noise = noise[:, 0:64]
        row_noise = noise[:, 64:96]

        def permute_scales(w, four_modules):
            nc.vector.tensor_copy(
                out=hidden_scales[:, w, four_modules, :].rearrange(
                    "p (h t m) -> p h m t", t=PACK, m=P
                ),
                in_=scales_loaded[:, w, four_modules, :].rearrange(
                    "p (h m t) -> p h m t", t=PACK, m=P
                ),
            )

        def permute_words(j, w):
            words = three.tile([P, HIDDEN], I32, align_bytes=64, name="words_%d" % w)
            hidden_words[j, w] = words
            nc.vector.tensor_copy(
                out=words[:].rearrange("p (h t m) -> p h m t", t=PACK, m=P),
                in_=hidden_loaded[j, w][:].rearrange("p (h m t) -> p h m t", t=PACK, m=P),
            )

        def turn_x1(j, part):
            if part == 0:
                x1_tile = two.tile([P, PACK * ROWS], BF16, align_bytes=64, name="x1_grouped")
                x1_grouped[j] = x1_tile
            grouped_words = x1_grouped[j][:].bitcast(F32).rearrange(
                "p (a b u) -> p a b u", a=ROW_TILES, u=2
            )
            first = 2 * part
            turned = work_psum.tile([P, 2, 2, P], F32, tag="work")
            for a in range(2):
                words = x1_sb[:, j, first + a, :].bitcast(F32)
                for u in range(2):
                    nc.tensor.transpose(
                        out=turned[:, a, u, :],
                        in_=words[:, u : FEATURES // 2 : 2],
                        identity=ident[:],
                    )
            nc.scalar.copy(
                out=grouped_words[:, first : first + 2, :, :],
                in_=turned[:].rearrange("p a u b -> p a b u"),
            )

        def spread_row_noise(j):
            spread = noise_psum_pool.tile([P, ROWS], F32, name="row_noise_all")
            row_noise_all[j] = spread
            for a in range(ROW_TILES):
                column = row_noise[:, MODULES * a + j : MODULES * a + j + 1]
                nc.tensor.transpose(
                    out=spread[:, P * a : P * (a + 1)],
                    in_=column.to_broadcast([P, P]),
                    identity=ident[:],
                )

        def quantise_x1(j):
            codes = two.tile([P, ROWS], U32, align_bytes=64, name="x1_codes")
            scales = two.tile([P, ROWS], U8, align_bytes=64, name="x1_scales")
            x1_codes[j] = codes
            x1_scales[j] = scales
            nc.vector.quantize_mx(
                out=codes[:].bitcast(FP8X4), scales=scales[:], in_=x1_grouped[j][:]
            )

        def hidden_pass(acc, half, w, t):
            j, h = divmod(half, 2)
            first = HALF_UNITS * h + P * t
            nc.tensor.matmul_mx(
                out=acc[:],
                lhsT=hidden_words[j, w][:, first : first + P].bitcast(FP8X4),
                lhsT_scale=hidden_scales[4 * (j % 4) : P, w, j // 4, first : first + P],
                rhs=x1_codes[j][:].bitcast(FP8X4),
                rhs_scale=x1_scales[j][:],
                start=True,
                stop=True,
            )

        def sigma_of_pair(n):
            half, late = divmod(n, 2)
            sig = four.tile([P, 2, ROWS], F32, name="sigma")
            sigma[n] = sig
            for i in range(2):
                t = 2 * late + i
                acc = sigma_psum.tile([P, ROWS], F32, tag="log_sigma")
                hidden_pass(acc, half, 1, t)
                nc.scalar.activation(
                    out=sig[:, i, :],
                    in_=acc[:],
                    func=ACT.Exp,
                    bias=vector_cols[:, t, 1, half : half + 1],
                    scale=1.0,
                )
                nc.gpsimd.tensor_scalar(
                    out=sig[:, i, :],
                    in0=sig[:, i, :],
                    scalar1=SIGMA_MAX,
                    scalar2=SIGMA_MIN,
                    op0=ALU.min,
                    op1=ALU.max,
                )

        def terms_of_pair(n):
            half, late = divmod(n, 2)
            j = half // 2
            for i in range(2):
                col = HALVES * (2 * late + i) + half
                term = six.tile([P, ROWS], F32, name="noise_term")
                terms[n, i] = term
                nc.vector.scalar_tensor_tensor(
                    out=term[:],
                    in0=sigma[n][:, i, :],
                    scalar=unit_noise[:, col : col + 1],
                    in1=row_noise_all[j][:],
                    op0=ALU.mult,
                    op1=ALU.mult,
                )

        def x2_of_pair(n):
            half, late = divmod(n, 2)
            if late == 0:
                units_tile = three.tile([P, PACK, ROWS], BF16, name="x2_units")
                x2_units[half] = units_tile
            accs = []
            for i in range(2):
                acc = mu_psum.tile([P, ROWS], F32, tag="mu")
                hidden_pass(acc, half, 0, 2 * late + i)
                accs.append(acc)
            for i in range(2):
                t = 2 * late + i
                nc.vector.scalar_tensor_tensor(
                    out=x2_units[half][:, t, :],
                    in0=accs[i][:],
                    scalar=vector_cols[:, t, 0, half : half + 1],
                    in1=terms[n, i][:],
                    op0=ALU.add,
                    op1=ALU.add,
                )

        def relu_and_group(half, part):
            if part == 0:
                x2_tile = two.tile([P, ROWS, PACK], BF16, align_bytes=64, name="x2_grouped")
                x2_grouped[half] = x2_tile
            rows = slice(ROWS // 2 * part, ROWS // 2 * (part + 1))
            by_row = x2_units[half][:, :, rows].rearrange(
                "p t (c i) -> p c t i", i=GROUP_ROWS
            )
            grouped = x2_grouped[half][:, rows, :].rearrange(
                "p (c i) t -> p c t i", i=GROUP_ROWS
            )
            if half == HALVES - 1 and part == 0:
                nc.vector.tensor_scalar_max(out=grouped, in0=by_row, scalar1=0.0)
            else:
                nc.scalar.activation(out=grouped, in_=by_row, func=ACT.Relu)

        def quantise_x2(half):
            j, g = divmod(half, 2)
            if g == 0:
                codes = two.tile([P, 2, ROWS], U32, align_bytes=64, name="x2_codes")
                scales = two.tile([P, 2, ROWS], U8, align_bytes=64, name="x2_scales")
                x2_codes[j] = codes
                x2_scales[j] = scales
            width = ROWS // 2 if half == HALVES - 1 else ROWS
            for first in range(0, ROWS, width):
                rows = slice(first, first + width)
                nc.vector.quantize_mx(
                    out=x2_codes[j][:, g, rows].bitcast(FP8X4),
                    scales=x2_scales[j][:, g, rows],
                    in_=x2_grouped[half][:, rows, :].rearrange("p b t -> p (b t)"),
                )

        def turn_head_bias():
            turned = work_psum.tile([P, P], BF16, tag="work")
            nc.tensor.transpose(out=turned[:], in_=head_rows[:], identity=ident_bf[:])
            nc.vector.tensor_copy(out=head_cols[:], in_=turned[:, 0 : 2 * MODULES])

        def head_by_output(j, w):
            acc = work_psum.tile([P, ROWS], F32, tag="work")
            for g in range(2):
                nc.tensor.matmul_mx(
                    out=acc[:],
                    lhsT=head_words[:, 2 * j + g, w, :].bitcast(FP8X4),
                    lhsT_scale=head_scales[:, 2 * j + g, w, :],
                    rhs=x2_codes[j][:, g, :].bitcast(FP8X4),
                    rhs_scale=x2_scales[j][:, g, :],
                    start=(g == 0),
                    stop=(g == 1),
                )
            outputs = two.tile([P, ROWS], F32, name="outputs_%d" % w)
            by_output[j, w] = outputs
            nc.scalar.activation(
                out=outputs[:],
                in_=acc[:],
                func=ACT.Identity,
                bias=head_cols[:, MODULES * w + j : MODULES * w + j + 1],
                scale=1.0,
            )
            if w == 1:
                nc.gpsimd.tensor_scalar(
                    out=outputs[:],
                    in0=outputs[:],
                    scalar1=LOG_STDEV_MAX,
                    scalar2=LOG_STDEV_MIN,
                    op0=ALU.min,
                    op1=ALU.max,
                )

        def store_head(j, w):
            out = (out_0, out_1)[w]
            turned = work_psum.tile([P, ROW_TILES, OUT], F32, tag="work")
            for a in range(ROW_TILES):
                nc.tensor.transpose(
                    out=turned[:, a, :],
                    in_=by_output[j, w][:, P * a : P * (a + 1)],
                    identity=ident[:],
                )
            by_row = two.tile([P, ROW_TILES, OUT], F32, name="by_row_%d" % w)
            nc.scalar.copy(out=by_row[:], in_=turned[:])
            nc.sync.dma_start(
                out=out[:, j, :].rearrange("(a p) o -> p a o", p=P), in_=by_row[:]
            )

        def last_heads():
            j = MODULES - 1
            bias = last_bias[:].rearrange("p w n -> p (w n)").unsqueeze(1)
            for first in (0, 2):
                acc = mu_psum.tile([P, 2, 2 * OUT], F32, tag="mu")
                for a in range(2):
                    rows = slice(P * (first + a), P * (first + a + 1))
                    for g in range(2):
                        nc.tensor.matmul_mx(
                            out=acc[:, a, :],
                            lhsT=x2_codes[j][:, g, rows].bitcast(FP8X4),
                            lhsT_scale=x2_scales[j][:, g, rows],
                            rhs=head_words[:, 2 * j + g, :, :]
                            .rearrange("p w n -> p (w n)")
                            .bitcast(FP8X4),
                            rhs_scale=head_scales[:, 2 * j + g, :, :].rearrange("p w n -> p (w n)"),
                            start=(g == 0),
                            stop=(g == 1),
                        )
                result = two.tile([P, 2, 2 * OUT], F32, name="result")
                nc.vector.tensor_tensor(
                    out=result[:], in0=acc[:], in1=bias.to_broadcast([P, 2, 2 * OUT]), op=ALU.add
                )
                rows = slice(P * first, P * (first + 2))
                nc.sync.dma_start(
                    out=out_0[rows, j, :].rearrange("(a p) o -> p a o", p=P),
                    in_=result[:, :, 0:OUT],
                )
                nc.vector.tensor_scalar(
                    out=result[:, :, OUT : 2 * OUT],
                    in0=result[:, :, OUT : 2 * OUT],
                    scalar1=LOG_STDEV_MIN,
                    scalar2=LOG_STDEV_MAX,
                    op0=ALU.max,
                    op1=ALU.min,
                )
                nc.sync.dma_start(
                    out=out_1[rows, j, :].rearrange("(a p) o -> p a o", p=P),
                    in_=result[:, :, OUT : 2 * OUT],
                )

        with tc.manual_schedule(
            engines={
                mybir.EngineType.PE,
                mybir.EngineType.DVE,
                mybir.EngineType.Activation,
            }
        ):
            for part in range(2):
                turn_x1(0, part)
            turn_vectors()
            permute_scales(1, 0)
            permute_words(0, 1)
            finish_noise()
            spread_row_noise(0)
            quantise_x1(0)
        nc.vector.tensor_copy(out=ident_bf[:], in_=ident[:])
        permute_scales(0, 0)
        permute_words(0, 0)
        for n in range(-2, PAIRS + 4):
            j, late = divmod(n, 4)
            running = 0 <= j and j + 1 < MODULES
            if 0 <= n + 1 < PAIRS:
                terms_of_pair(n + 1)
            if 0 <= n < PAIRS:
                x2_of_pair(n)
            if n + 2 < PAIRS:
                sigma_of_pair(n + 2)
            if 0 <= n - 2 < PAIRS:
                relu_and_group((n - 2) // 2, n % 2)
            if n == -2:
                for part in range(2):
                    turn_x1(1, part)
            if n == 5:
                turn_head_bias()
            if late == 0:
                if 0 <= n // 2 - 2:
                    quantise_x2(n // 2 - 2)
                if 0 <= j - 2 < MODULES - 1:
                    head_by_output(j - 2, 1)
                if running:
                    quantise_x1(j + 1)
            if late == 1:
                if 0 <= j and j + 2 < MODULES:
                    turn_x1(j + 2, 0)
                if 0 <= j - 2 < MODULES - 1:
                    store_head(j - 2, 0)
                if running:
                    permute_words(j + 1, 0)
                    if j + 1 == 4:
                        permute_scales(0, 1)
                    spread_row_noise(j + 1)
            if late == 2:
                if 0 <= n // 2 - 2:
                    quantise_x2(n // 2 - 2)
                if 0 <= j and j + 2 < MODULES:
                    turn_x1(j + 2, 1)
                if 0 <= j - 2 < MODULES - 1:
                    store_head(j - 2, 1)
            if late == 3:
                if 0 <= j - 1 < MODULES - 1:
                    head_by_output(j - 1, 0)
                if j + 2 < MODULES:
                    permute_words(j + 2, 1)
                    if j + 2 == 4:
                        permute_scales(1, 1)
        last_heads()
